import numpy as np
import ml_dtypes


def mxq(x, axis, fmt="e4m3"):
    dtype, down = {"e4m3": (ml_dtypes.float8_e4m3fn, 7), "e5m2": (ml_dtypes.float8_e5m2, 14)}[fmt]
    v = np.moveaxis(np.asarray(x, np.float32).astype(ml_dtypes.bfloat16).astype(np.float64), axis, -1)
    blocks = v.reshape(v.shape[:-1] + (-1, 32))
    amax = np.abs(blocks).max(-1, keepdims=True)
    byte = np.maximum(np.where(amax > 0, np.frexp(amax)[1] - 1 + 127, 0) - down, 1)
    scale = np.exp2(byte - 127.0)
    codes = (blocks / scale).astype(np.float32).astype(dtype).astype(np.float64)
    return np.moveaxis((codes * scale).reshape(v.shape), -1, axis)


WIDE = False


def mx_kscale(k):
    if not WIDE:
        return np.ones(k)
    levels = np.array([10, -10, 5, -5, 0])
    if k % 512:
        return np.exp2(np.random.permutation(np.resize(levels, k // 32))).repeat(32)
    a = np.empty((k // 512, 16))
    for p in range(k // 512):
        a[p, :8] = np.random.permutation(np.resize(levels, 8))
        for g in range(8):
            far = levels[np.abs(levels - a[p, g]) >= 10]
            a[p, g + 8] = far[np.random.randint(len(far))]
    return np.exp2(a.ravel()).repeat(32)


BF16 = ml_dtypes.bfloat16


def bf(x):
    return np.asarray(x, np.float32).astype(BF16)


def f64(x):
    return np.asarray(x).astype(np.float64)


B, IN, H = 128, 7680, 512
D = IN + H
LN_EPS = 1e-5
DIV_EPS = 1e-6


def sigmoid(v):
    return 1.0 / (1.0 + np.exp(-v))


def setup_inputs():
    s = mx_kscale(D)
    d = {"x": bf(np.random.standard_normal((B, IN)) * s[:IN]),
         "h_prev": bf(np.random.standard_normal((B, H)) * s[IN:]),
         "c_prev": bf(np.random.standard_normal((B, H))),
         "n_prev": bf(np.random.uniform(0.0, 1.0, (B, H))),
         "m_prev": bf(np.random.uniform(0.0, 1.0, (B, H)))}
    for g in "ifoz":
        d["W" + g] = bf(np.random.standard_normal((H, D)) * 0.6 / np.sqrt(D) / s)
        d["b" + g] = bf(np.random.standard_normal(H) * 0.3)
    d["ln_gamma"] = bf(1.0 + 0.1 * np.random.standard_normal(H))
    d["ln_beta"] = bf(0.1 * np.random.standard_normal(H))
    return d


def reference(x, h_prev, c_prev, n_prev, m_prev, Wi, bi, Wf, bf, Wo, bo, Wz, bz, ln_gamma, ln_beta):
    combined = np.concatenate([f64(x), f64(h_prev)], axis=1)
    W = np.stack([f64(Wi), f64(Wf), f64(Wo), f64(Wz)], axis=0)
    b = np.stack([f64(bi), f64(bf), f64(bo), f64(bz)], axis=0)
    gates = (mxq(combined, 1, "e4m3") @ mxq(W, 2, "e4m3").transpose(0, 2, 1)) + b[:, None, :]
    i_t = np.exp(gates[0])
    f_t = sigmoid(gates[1])
    o_t = sigmoid(gates[2])
    z_t = np.tanh(gates[3])
    c_t = f_t * f64(c_prev) + i_t * z_t
    n_t = f_t * f64(n_prev) + i_t
    m_t = np.maximum(f_t * f64(m_prev), np.abs(i_t * z_t))
    h = o_t * (c_t / (n_t + DIV_EPS))
    mu = np.mean(h, axis=-1, keepdims=True)
    var = np.mean(np.square(h - mu), axis=-1, keepdims=True)
    h_t = (h - mu) * (1.0 / np.sqrt(var + LN_EPS)) * f64(ln_gamma) + f64(ln_beta)
    return (h_t, c_t, n_t, m_t)

@@ -1,0 +1,332 @@
+from contextlib import ExitStack
+
+import concourse.mybir as mybir
+from concourse.masks import make_identity
+
+F32 = mybir.dt.float32
+BF16 = mybir.dt.bfloat16
+I32 = mybir.dt.int32
+U32 = mybir.dt.uint32
+U8 = mybir.dt.uint8
+FP8X4 = mybir.dt.float8_e4m3fn_x4
+ALU = mybir.AluOpType
+ACT = mybir.ActivationFunctionType
+
+P = 128
+IN = 7680
+H = 512
+D = IN + H
+LN_EPS = 1e-5
+DIV_EPS = 1e-6
+
+PACK = 4
+K_PASS = P * PACK
+PASSES = D // K_PASS
+BANK_WORDS = 512
+PASSES_PER_BANK = BANK_WORDS // (2 * P)
+
+GATES = ("f", "i", "z", "o")
+BLOCKS_PER_GATE = H // P
+BLOCKS = len(GATES) * BLOCKS_PER_GATE
+
+TRANSPOSE_BANKS = 6
+PREFETCH = 8
+MULTIPLY_LAG = 2
+
+FLOPS = 2 * P * D * len(GATES) * H
+
+
+def piece_sizes(taper):
+    sizes = [PASSES // 2]
+    rest = PASSES // 2
+    while taper and rest > PASSES_PER_BANK:
+        rest = rest // 2
+        sizes.append(rest)
+    sizes.append(rest)
+    return sizes
+
+
+def tile_slstmcell_k_kernel(
+    tc, x, h_prev, c_prev, n_prev, m_prev, Wi, bi, Wf, bf, Wo, bo, Wz, bz, ln_gamma, ln_beta,
+    out_0, out_1, out_2, out_3,
+):
+    nc = tc.nc
+    weights = {"f": Wf, "i": Wi, "z": Wz, "o": Wo}
+    row_vectors = {"f": bf, "i": bi, "z": bz, "o": bo, "gamma": ln_gamma, "beta": ln_beta}
+    previous = {"c": c_prev, "n": n_prev, "m": m_prev}
+
+    with ExitStack() as ctx:
+        ctx.enter_context(tc.manual_schedule())
+        keep = ctx.enter_context(tc.tile_pool(name="keep", bufs=1))
+        raw_pool = ctx.enter_context(tc.tile_pool(name="raw", bufs=PREFETCH + 2))
+        grouped_pool = ctx.enter_context(tc.tile_pool(name="grouped", bufs=5))
+        quantised_pool = ctx.enter_context(tc.tile_pool(name="quantised", bufs=5))
+        small_pool = ctx.enter_context(tc.tile_pool(name="small", bufs=3))
+        bank_pool = ctx.enter_context(tc.psum_pool(name="banks", bufs=TRANSPOSE_BANKS))
+        sum_pool = ctx.enter_context(tc.psum_pool(name="sums", bufs=2))
+
+        identity = keep.tile([P, P], F32, name="identity")
+        make_identity(nc, identity[:])
+        ones = keep.tile([P, P], BF16, name="ones")
+        nc.vector.memset(ones[:], 1.0)
+        minus_half = keep.tile([P, 1], F32, name="minus_half")
+        nc.vector.memset(minus_half[:], -0.5)
+        vector_rows = keep.tile([P, len(row_vectors) * H], BF16, name="vector_rows")
+        nc.vector.memset(vector_rows[:].bitcast(I32), 0)
+        table_warmer = keep.tile([P, 1], F32, name="table_warmer")
+        nc.scalar.activation(out=table_warmer[:], in_=minus_half[:], func=ACT.Tanh)
+
+        for v, name in enumerate(row_vectors):
+            nc.gpsimd.dma_start(
+                out=vector_rows[0:1, v * H : (v + 1) * H], in_=row_vectors[name].unsqueeze(0)
+            )
+        previous_bf16 = {}
+        for name in previous:
+            previous_bf16[name] = keep.tile([P, H], BF16, name="previous_" + name)
+            nc.gpsimd.dma_start(out=previous_bf16[name][:], in_=previous[name])
+
+        pieces = []
+        for block in range(BLOCKS):
+            first_pass = 0
+            for n_passes in piece_sizes(block == BLOCKS - 1):
+                pieces.append((block, first_pass, n_passes))
+                first_pass += n_passes
+
+        raw_at = {}
+
+        def load_rows(block, first_pass, n_passes, sources):
+            raw = raw_pool.tile([P, n_passes * K_PASS], BF16, name="raw")
+            column = 0
+            for source in sources:
+                nc.sync.dma_start(out=raw[:, column : column + source.shape[1]], in_=source)
+                column += source.shape[1]
+            for q in range(n_passes):
+                raw_at[(block, first_pass + q)] = (raw, q * K_PASS)
+
+        def load_weight_piece(t):
+            block, first_pass, n_passes = pieces[t]
+            gate, j = divmod(block, BLOCKS_PER_GATE)
+            k_range = slice(first_pass * K_PASS, (first_pass + n_passes) * K_PASS)
+            load_rows(block, first_pass, n_passes, [weights[GATES[gate]][j * P : (j + 1) * P, k_range]])
+
+        COMBINED = -1
+        half_k = D // 2
+        load_rows(COMBINED, 0, PASSES // 2, [x[:, 0:half_k]])
+        load_rows(COMBINED, PASSES // 2, PASSES // 2, [x[:, half_k:IN], h_prev])
+        for t in range(PREFETCH):
+            load_weight_piece(t)
+
+        def transpose_piece(block, first_pass, n_passes):
+            grouped = grouped_pool.tile([P, n_passes * K_PASS], BF16, name="grouped", align_bytes=64)
+            grouped_words = grouped[:].bitcast(F32)
+            n_banks = n_passes // PASSES_PER_BANK
+            left_for_vector = None
+            for b in range(n_banks):
+                bank = bank_pool.tile([P, 2, BANK_WORDS // 2], F32, name="bank")
+                for g in range(PASSES_PER_BANK):
+                    raw, column = raw_at[(block, first_pass + b * PASSES_PER_BANK + g)]
+                    pass_words = raw[:, column : column + K_PASS].bitcast(F32)
+                    for u in range(2):
+                        nc.tensor.transpose(
+                            bank[:, u, g * P : (g + 1) * P],
+                            pass_words[:, u : 2 * P : 2],
+                            identity[:],
+                        )
+                out = grouped_words[:, b * BANK_WORDS : (b + 1) * BANK_WORDS].rearrange(
+                    "p (c u) -> p c u", u=2
+                )
+                in_ = bank[:].rearrange("p u c -> p c u")
+                if b == n_banks - 1 and first_pass == 0:
+                    left_for_vector = (out, in_)
+                else:
+                    nc.scalar.copy(out=out, in_=in_)
+            return grouped, left_for_vector
+
+        def vector_empties(left_for_vector):
+            if left_for_vector is not None:
+                nc.vector.tensor_copy(out=left_for_vector[0], in_=left_for_vector[1])
+
+        def quantise_piece(grouped, codes, scales):
+            nc.vector.quantize_mx(out=codes.bitcast(FP8X4), scales=scales, in_=grouped[:])
+
+        x_codes = keep.tile([P, PASSES * P], U32, name="x_codes", align_bytes=64)
+        x_scales = keep.tile([P, PASSES * P], U8, name="x_scales", align_bytes=64)
+        for first_pass in (0, PASSES // 2):
+            grouped, left_for_vector = transpose_piece(COMBINED, first_pass, PASSES // 2)
+            vector_empties(left_for_vector)
+            words = slice(first_pass * P, (first_pass + PASSES // 2) * P)
+            quantise_piece(grouped, x_codes[:, words], x_scales[:, words])
+
+        spread = {}
+
+        def spread_row_vectors():
+            names = list(row_vectors)
+            for first in range(0, len(names), 2):
+                bank = bank_pool.tile([P, 2 * H], BF16, name="bank")
+                pair = keep.tile([P, 2 * H], BF16, name="spread%d" % first)
+                for v in (0, 1):
+                    nc.tensor.matmul(
+                        out=bank[:, v * H : (v + 1) * H], lhsT=ones[:],
+                        rhs=vector_rows[:, (first + v) * H : (first + v + 1) * H],
+                        start=True, stop=True,
+                    )
+                    spread[names[first + v]] = pair[:, v * H : (v + 1) * H]
+                nc.vector.tensor_copy(out=pair[:], in_=bank[:])
+
+        half_previous = {}
+        for name in previous:
+            half_previous[name] = keep.tile([P, H], F32, name="half_previous_" + name)
+            nc.gpsimd.tensor_scalar(
+                out=half_previous[name][:], in0=previous_bf16[name][:],
+                scalar1=0.5, scalar2=0.0, op0=ALU.mult, op1=ALU.add,
+            )
+
+        full = {}
+        for name in (
+            "tanh_f", "f_c", "f_n", "f_m", "i", "denominator", "reciprocal", "n_t", "z", "i_z",
+            "larger", "c_t", "m_t", "half_ratio", "tanh_o", "h", "centred", "h_t",
+        ):
+            full[name] = keep.tile([P, H], F32, name=name)
+        stats = keep.tile([P, BLOCKS_PER_GATE, 6], F32, name="stats")
+        function_of = {"f": ACT.Tanh, "i": ACT.Exp, "z": ACT.Tanh, "o": ACT.Tanh}
+        scale_of = {"f": 0.5, "i": 1.0, "z": 1.0, "o": 0.5}
+        result_of = {"f": "tanh_f", "i": "i", "z": "z", "o": "tanh_o"}
+
+        def gate_and_columns(block):
+            gate, j = divmod(block, BLOCKS_PER_GATE)
+            return GATES[gate], j, slice(j * P, (j + 1) * P)
+
+        def add_bias(block):
+            gate, j, cols = gate_and_columns(block)
+            biased[block] = small_pool.tile([P, P], F32, name="biased")
+            nc.vector.tensor_add(out=biased[block][:], in0=sums[block][:], in1=spread[gate][:, cols])
+
+        def apply_function(block):
+            gate, j, cols = gate_and_columns(block)
+            nc.scalar.activation(
+                out=full[result_of[gate]][:, cols], in_=biased[block][:],
+                func=function_of[gate], scale=scale_of[gate],
+            )
+
+        def combine(block):
+            gate, j, cols = gate_and_columns(block)
+            if gate == "f":
+                for name in previous:
+                    nc.vector.scalar_tensor_tensor(
+                        out=full["f_" + name][:, cols], in0=full["tanh_f"][:, cols], scalar=1.0,
+                        in1=half_previous[name][:, cols], op0=ALU.add, op1=ALU.mult,
+                    )
+            if gate == "i":
+                nc.vector.scalar_tensor_tensor(
+                    out=full["denominator"][:, cols], in0=full["i"][:, cols], scalar=DIV_EPS,
+                    in1=full["f_n"][:, cols], op0=ALU.add, op1=ALU.add,
+                )
+                nc.vector.tensor_add(
+                    out=full["n_t"][:, cols], in0=full["f_n"][:, cols], in1=full["i"][:, cols]
+                )
+                nc.vector.reciprocal(out=full["reciprocal"][:, cols], in_=full["denominator"][:, cols])
+            if gate == "z":
+                nc.vector.tensor_mul(
+                    out=full["i_z"][:, cols], in0=full["i"][:, cols], in1=full["z"][:, cols]
+                )
+                nc.vector.tensor_max(
+                    out=full["larger"][:, cols], in0=full["f_m"][:, cols], in1=full["i_z"][:, cols]
+                )
+                nc.vector.tensor_add(
+                    out=full["c_t"][:, cols], in0=full["f_c"][:, cols], in1=full["i_z"][:, cols]
+                )
+                nc.vector.scalar_tensor_tensor(
+                    out=full["m_t"][:, cols], in0=full["i_z"][:, cols], scalar=-1.0,
+                    in1=full["larger"][:, cols], op0=ALU.mult, op1=ALU.max,
+                )
+                nc.vector.scalar_tensor_tensor(
+                    out=full["half_ratio"][:, cols], in0=full["c_t"][:, cols], scalar=0.5,
+                    in1=full["reciprocal"][:, cols], op0=ALU.mult, op1=ALU.mult,
+                )
+                if j == BLOCKS_PER_GATE - 1:
+                    nc.sync.dma_start(out=out_1, in_=full["c_t"][:])
+                    nc.sync.dma_start(out=out_2, in_=full["n_t"][:])
+                    nc.sync.dma_start(out=out_3, in_=full["m_t"][:])
+            if gate == "o":
+                nc.vector.scalar_tensor_tensor(
+                    out=full["h"][:, cols], in0=full["tanh_o"][:, cols], scalar=1.0,
+                    in1=full["half_ratio"][:, cols], op0=ALU.add, op1=ALU.mult,
+                )
+                nc.vector.bn_stats(out=stats[:, j, :], in_=full["h"][:, cols])
+
+
+        units = [[t] for t in range(len(pieces)) if pieces[t][0] < BLOCKS - 1]
+        units.append([t for t in range(len(pieces)) if pieces[t][0] == BLOCKS - 1])
+
+        def unit(number):
+            return units[number] if 0 <= number < len(units) else []
+
+        def finished_block(number):
+            for t in unit(number):
+                if pieces[t][1] + pieces[t][2] == PASSES:
+                    return pieces[t][0]
+            return None
+
+        grouped_of = {}
+        codes_of = {}
+        scales_of = {}
+        sums = {}
+        biased = {}
+        for step in range(len(units) + MULTIPLY_LAG + 2):
+            left_for_vector = None
+            for t in unit(step):
+                block, first_pass, n_passes = pieces[t]
+                if t + PREFETCH < len(pieces):
+                    load_weight_piece(t + PREFETCH)
+                grouped_of[t], left = transpose_piece(block, first_pass, n_passes)
+                if left is not None:
+                    left_for_vector = left
+
+            for t in unit(step - 1):
+                n_words = pieces[t][2] * P
+                codes_of[t] = quantised_pool.tile([P, n_words], U32, name="w_codes", align_bytes=64)
+                scales_of[t] = quantised_pool.tile([P, n_words], U8, name="w_scales", align_bytes=64)
+                quantise_piece(grouped_of[t], codes_of[t][:], scales_of[t][:])
+
+            if step == MULTIPLY_LAG:
+                spread_row_vectors()
+
+            for t in unit(step - MULTIPLY_LAG):
+                block, first_pass, n_passes = pieces[t]
+                if first_pass == 0:
+                    sums[block] = sum_pool.tile([P, P], F32, name="sums")
+                for q in range(n_passes):
+                    x_words = slice((first_pass + q) * P, (first_pass + q + 1) * P)
+                    w_words = slice(q * P, (q + 1) * P)
+                    nc.tensor.matmul_mx(
+                        out=sums[block][:],
+                        lhsT=x_codes[:, x_words].bitcast(FP8X4),
+                        lhsT_scale=x_scales[:, x_words],
+                        rhs=codes_of[t][:, w_words].bitcast(FP8X4),
+                        rhs_scale=scales_of[t][:, w_words],
+                        start=(first_pass + q == 0),
+                        stop=(first_pass + q == PASSES - 1),
+                    )
+
+            if finished_block(step - MULTIPLY_LAG - 1) is not None:
+                add_bias(finished_block(step - MULTIPLY_LAG - 1))
+                apply_function(finished_block(step - MULTIPLY_LAG - 1))
+            if finished_block(step - MULTIPLY_LAG - 2) is not None:
+                combine(finished_block(step - MULTIPLY_LAG - 2))
+            vector_empties(left_for_vector)
+
+        mean_var = keep.tile([P, 2], F32, name="mean_var")
+        nc.vector.bn_aggr(out=mean_var[:], in_=stats[:].rearrange("p j s -> p (j s)"))
+        var_eps = keep.tile([P, 1], F32, name="var_eps")
+        nc.vector.tensor_scalar_add(out=var_eps[:], in0=mean_var[:, 1:2], scalar1=LN_EPS)
+        inv_std = keep.tile([P, 1], F32, name="inv_std")
+        nc.gpsimd.tensor_tensor(out=inv_std[:], in0=var_eps[:], in1=minus_half[:], op=ALU.pow)
+        nc.vector.scalar_tensor_tensor(
+            out=full["centred"][:], in0=full["h"][:], scalar=mean_var[:, 0:1],
+            in1=spread["gamma"], op0=ALU.subtract, op1=ALU.mult,
+        )
+        nc.vector.scalar_tensor_tensor(
+            out=full["h_t"][:], in0=full["centred"][:], scalar=inv_std[:],
+            in1=spread["beta"], op0=ALU.mult, op1=ALU.add,
+        )
+        nc.sync.dma_start(out=out_0, in_=full["h_t"][:])

@@ -22,28 +22,24 @@ DIV_EPS = 1e-6
 PACK = 4
 K_PASS = P * PACK
 PASSES = D // K_PASS
-BANK_WORDS = 512
-PASSES_PER_BANK = BANK_WORDS // (2 * P)
-
-GATES = ("f", "i", "z", "o")
+PASS_PAIRS = K_PASS // 2
 BLOCKS_PER_GATE = H // P
-BLOCKS = len(GATES) * BLOCKS_PER_GATE
+UNITS_PER_BANK = 2
+
+WIDE_GATES = ("f", "i", "z")
+NARROW_GATE = "o"
+WIDE_LOAD_PASSES = 4
+WIDE_STEP_PASSES = 2
+NARROW_STEP_PASSES = 8
+WIDE_SPLIT = (1,)
+NARROW_SORTED = 4
 
 TRANSPOSE_BANKS = 6
-PREFETCH = 8
+RAW_BUFS = 10
+X_PARTS = (2, 4, 6, 4)
 MULTIPLY_LAG = 2
 
-FLOPS = 2 * P * D * len(GATES) * H
-
-
-def piece_sizes(taper):
-    sizes = [PASSES // 2]
-    rest = PASSES // 2
-    while taper and rest > PASSES_PER_BANK:
-        rest = rest // 2
-        sizes.append(rest)
-    sizes.append(rest)
-    return sizes
+FLOPS = 2 * P * D * 4 * H
 
 
 def tile_slstmcell_k_kernel(
@@ -58,12 +54,78 @@ def tile_slstmcell_k_kernel(
     with ExitStack() as ctx:
         ctx.enter_context(tc.manual_schedule())
         keep = ctx.enter_context(tc.tile_pool(name="keep", bufs=1))
-        raw_pool = ctx.enter_context(tc.tile_pool(name="raw", bufs=PREFETCH + 2))
-        grouped_pool = ctx.enter_context(tc.tile_pool(name="grouped", bufs=5))
-        quantised_pool = ctx.enter_context(tc.tile_pool(name="quantised", bufs=5))
-        small_pool = ctx.enter_context(tc.tile_pool(name="small", bufs=3))
+        raw_pool = ctx.enter_context(tc.tile_pool(name="raw", bufs=RAW_BUFS))
+        sorted_pool = ctx.enter_context(tc.tile_pool(name="sorted", bufs=4))
+        grouped_pool = ctx.enter_context(tc.tile_pool(name="grouped", bufs=4))
+        quantised_pool = ctx.enter_context(tc.tile_pool(name="quantised", bufs=3))
+        small_pool = ctx.enter_context(tc.tile_pool(name="small", bufs=2))
         bank_pool = ctx.enter_context(tc.psum_pool(name="banks", bufs=TRANSPOSE_BANKS))
         sum_pool = ctx.enter_context(tc.psum_pool(name="sums", bufs=2))
+
+        loads = []
+        steps = []
+        for gate in WIDE_GATES:
+            for first in range(0, PASSES, WIDE_LOAD_PASSES):
+                k_range = slice(first * K_PASS, (first + WIDE_LOAD_PASSES) * K_PASS)
+                base = len(loads)
+                for pair in range(2):
+                    rows = slice(pair * 2 * P, (pair + 1) * 2 * P)
+                    loads.append((2 * WIDE_LOAD_PASSES * K_PASS, weights[gate][rows, k_range], 2))
+                for sub in range(WIDE_LOAD_PASSES // WIDE_STEP_PASSES):
+                    n_sorted = WIDE_SPLIT[len(steps) % len(WIDE_SPLIT)]
+                    units = []
+                    for g in range(WIDE_STEP_PASSES):
+                        for r in range(BLOCKS_PER_GATE):
+                            pass_in_load = sub * WIDE_STEP_PASSES + g
+                            units.append((base + r // 2, ((r % 2) * WIDE_LOAD_PASSES + pass_in_load) * PASS_PAIRS))
+                    steps.append({
+                        "gate": gate, "block": None, "first": first + sub * WIDE_STEP_PASSES,
+                        "passes": WIDE_STEP_PASSES, "units": units,
+                        "sort": [(base + q, 2, sub * WIDE_STEP_PASSES, WIDE_STEP_PASSES, WIDE_LOAD_PASSES) for q in range(n_sorted)],
+                    })
+        for block in range(BLOCKS_PER_GATE):
+            last = block == BLOCKS_PER_GATE - 1
+            first = 0
+            for n in (8, 4, 2, 2) if last else (8, 8):
+                rows = slice(block * P, (block + 1) * P)
+                k_range = slice(first * K_PASS, (first + n) * K_PASS)
+                n_sorted = n * NARROW_SORTED // NARROW_STEP_PASSES if n == NARROW_STEP_PASSES else 0
+                steps.append({
+                    "gate": NARROW_GATE, "block": block, "first": first, "passes": n,
+                    "units": [(len(loads), g * PASS_PAIRS) for g in range(n)],
+                    "sort": [(len(loads), 1, 0, n_sorted, n)] if n_sorted else [],
+                })
+                loads.append((n * K_PASS, weights[NARROW_GATE][rows, k_range], 1))
+                first += n
+
+        raw_of = {}
+
+        def load(t):
+            if t < len(loads):
+                width, source, n_rows = loads[t]
+                raw = raw_pool.tile([P, width], BF16, name="raw")
+                raw_of[t] = raw
+                if n_rows == 1:
+                    nc.sync.dma_start(out=raw[:], in_=source)
+                else:
+                    nc.sync.dma_start(
+                        out=raw[:].rearrange("p (r k) -> p r k", r=n_rows),
+                        in_=source.rearrange("(r p) k -> p r k", r=n_rows),
+                    )
+
+        x_raw = []
+        first = 0
+        for n in X_PARTS:
+            raw = raw_pool.tile([P, n * K_PASS], BF16, name="raw")
+            k0 = first * K_PASS
+            k1 = min((first + n) * K_PASS, IN)
+            nc.sync.dma_start(out=raw[:, 0 : k1 - k0], in_=x[:, k0:k1])
+            if k1 == IN:
+                nc.sync.dma_start(out=raw[:, k1 - k0 : n * K_PASS], in_=h_prev)
+            x_raw.append((raw, first, n))
+            first += n
+        for number in range(RAW_BUFS - len(X_PARTS)):
+            load(number)
 
         identity = keep.tile([P, P], F32, name="identity")
         make_identity(nc, identity[:])
@@ -84,78 +146,86 @@ def tile_slstmcell_k_kernel(
         for name in previous:
             previous_bf16[name] = keep.tile([P, H], BF16, name="previous_" + name)
             nc.gpsimd.dma_start(out=previous_bf16[name][:], in_=previous[name])
+        half_previous = {}
+        for name in previous:
+            half_previous[name] = keep.tile([P, H], F32, name="half_previous_" + name)
+            nc.gpsimd.tensor_scalar(
+                out=half_previous[name][:], in0=previous_bf16[name][:],
+                scalar1=0.5, scalar2=0.0, op0=ALU.mult, op1=ALU.add,
+            )
 
-        pieces = []
-        for block in range(BLOCKS):
-            first_pass = 0
-            for n_passes in piece_sizes(block == BLOCKS - 1):
-                pieces.append((block, first_pass, n_passes))
-                first_pass += n_passes
+        def sort_words(raw, n_rows, first, n, pitch):
+            half = n_rows * n * P
+            out_tile = sorted_pool.tile([P, 2 * half], F32, name="sorted")
+            in_ = raw[:].bitcast(F32).rearrange("p (r n u) -> p u r n", r=n_rows, u=2)
+            in_ = in_[:, :, :, first * P : (first + n) * P]
+            nc.vector.tensor_copy(
+                out=out_tile[:].rearrange("p (u r n) -> p u r n", u=2, r=n_rows), in_=in_
+            )
+            places = {}
+            for r in range(n_rows):
+                for g in range(n):
+                    places[(r * pitch + first + g) * PASS_PAIRS] = (out_tile, (r * n + g) * P, half)
+            return places
 
-        raw_at = {}
-
-        def load_rows(block, first_pass, n_passes, sources):
-            raw = raw_pool.tile([P, n_passes * K_PASS], BF16, name="raw")
-            column = 0
-            for source in sources:
-                nc.sync.dma_start(out=raw[:, column : column + source.shape[1]], in_=source)
-                column += source.shape[1]
-            for q in range(n_passes):
-                raw_at[(block, first_pass + q)] = (raw, q * K_PASS)
-
-        def load_weight_piece(t):
-            block, first_pass, n_passes = pieces[t]
-            gate, j = divmod(block, BLOCKS_PER_GATE)
-            k_range = slice(first_pass * K_PASS, (first_pass + n_passes) * K_PASS)
-            load_rows(block, first_pass, n_passes, [weights[GATES[gate]][j * P : (j + 1) * P, k_range]])
-
-        COMBINED = -1
-        half_k = D // 2
-        load_rows(COMBINED, 0, PASSES // 2, [x[:, 0:half_k]])
-        load_rows(COMBINED, PASSES // 2, PASSES // 2, [x[:, half_k:IN], h_prev])
-        for t in range(PREFETCH):
-            load_weight_piece(t)
-
-        def transpose_piece(block, first_pass, n_passes):
-            grouped = grouped_pool.tile([P, n_passes * K_PASS], BF16, name="grouped", align_bytes=64)
+        def transpose_units(sources):
+            grouped = grouped_pool.tile([P, len(sources) * K_PASS], BF16, name="grouped", align_bytes=64)
             grouped_words = grouped[:].bitcast(F32)
-            n_banks = n_passes // PASSES_PER_BANK
-            left_for_vector = None
-            for b in range(n_banks):
-                bank = bank_pool.tile([P, 2, BANK_WORDS // 2], F32, name="bank")
-                for g in range(PASSES_PER_BANK):
-                    raw, column = raw_at[(block, first_pass + b * PASSES_PER_BANK + g)]
-                    pass_words = raw[:, column : column + K_PASS].bitcast(F32)
+            for b in range(len(sources) // UNITS_PER_BANK):
+                bank = bank_pool.tile([P, 2, UNITS_PER_BANK * P], F32, name="bank")
+                for s in range(UNITS_PER_BANK):
+                    tile, column, half = sources[b * UNITS_PER_BANK + s]
                     for u in range(2):
-                        nc.tensor.transpose(
-                            bank[:, u, g * P : (g + 1) * P],
-                            pass_words[:, u : 2 * P : 2],
-                            identity[:],
-                        )
-                out = grouped_words[:, b * BANK_WORDS : (b + 1) * BANK_WORDS].rearrange(
-                    "p (c u) -> p c u", u=2
+                        if half is None:
+                            words = tile[:].bitcast(F32)[:, column + u : column + PASS_PAIRS : 2]
+                        else:
+                            words = tile[:, u * half + column : u * half + column + P]
+                        nc.tensor.transpose(bank[:, u, s * P : (s + 1) * P], words, identity[:])
+                span = UNITS_PER_BANK * PASS_PAIRS
+                nc.scalar.copy(
+                    out=grouped_words[:, b * span : (b + 1) * span].rearrange("p (c u) -> p c u", u=2),
+                    in_=bank[:].rearrange("p u c -> p c u"),
                 )
-                in_ = bank[:].rearrange("p u c -> p c u")
-                if b == n_banks - 1 and first_pass == 0:
-                    left_for_vector = (out, in_)
-                else:
-                    nc.scalar.copy(out=out, in_=in_)
-            return grouped, left_for_vector
+            return grouped
 
-        def vector_empties(left_for_vector):
-            if left_for_vector is not None:
-                nc.vector.tensor_copy(out=left_for_vector[0], in_=left_for_vector[1])
-
-        def quantise_piece(grouped, codes, scales):
+        def quantise(grouped, codes, scales):
             nc.vector.quantize_mx(out=codes.bitcast(FP8X4), scales=scales, in_=grouped[:])
+
+        places_of = {}
+
+        def sort_step(t):
+            if t < len(steps):
+                for number, n_rows, first, n, pitch in steps[t]["sort"]:
+                    places_of[(t, number)] = sort_words(raw_of[number], n_rows, first, n, pitch)
 
         x_codes = keep.tile([P, PASSES * P], U32, name="x_codes", align_bytes=64)
         x_scales = keep.tile([P, PASSES * P], U8, name="x_scales", align_bytes=64)
-        for first_pass in (0, PASSES // 2):
-            grouped, left_for_vector = transpose_piece(COMBINED, first_pass, PASSES // 2)
-            vector_empties(left_for_vector)
-            words = slice(first_pass * P, (first_pass + PASSES // 2) * P)
-            quantise_piece(grouped, x_codes[:, words], x_scales[:, words])
+
+        def quantise_x(grouped, first, n):
+            a = 0
+            while a < n:
+                size = 4 if n - a >= 4 else 2
+                words = slice((first + a) * P, (first + a + size) * P)
+                nc.vector.quantize_mx(
+                    out=x_codes[:, words].bitcast(FP8X4), scales=x_scales[:, words],
+                    in_=grouped[:, a * K_PASS : (a + size) * K_PASS],
+                )
+                a += size
+
+        places = {}
+        grouped_before = None
+        for part, (raw, first, n) in enumerate(x_raw):
+            grouped = transpose_units(
+                [places.get(g * PASS_PAIRS, (raw, g * PASS_PAIRS, None)) for g in range(n)]
+            )
+            if part + 1 < len(x_raw):
+                places = sort_words(x_raw[part + 1][0], 1, 0, x_raw[part + 1][2], x_raw[part + 1][2])
+            else:
+                sort_step(0)
+            if grouped_before is not None:
+                quantise_x(grouped_before, x_raw[part - 1][1], x_raw[part - 1][2])
+            grouped_before = grouped
+        quantise_x(grouped_before, x_raw[-1][1], x_raw[-1][2])
 
         spread = {}
 
@@ -173,147 +243,149 @@ def tile_slstmcell_k_kernel(
                     spread[names[first + v]] = pair[:, v * H : (v + 1) * H]
                 nc.vector.tensor_copy(out=pair[:], in_=bank[:])
 
-        half_previous = {}
-        for name in previous:
-            half_previous[name] = keep.tile([P, H], F32, name="half_previous_" + name)
-            nc.gpsimd.tensor_scalar(
-                out=half_previous[name][:], in0=previous_bf16[name][:],
-                scalar1=0.5, scalar2=0.0, op0=ALU.mult, op1=ALU.add,
-            )
-
         full = {}
         for name in (
-            "tanh_f", "f_c", "f_n", "f_m", "i", "denominator", "reciprocal", "n_t", "z", "i_z",
-            "larger", "c_t", "m_t", "half_ratio", "tanh_o", "h", "centred", "h_t",
+            "act_f", "act_i", "act_z", "act_o", "f_c", "f_n", "f_m", "denominator", "reciprocal", "n_t", "i_z",
+            "larger", "c_t", "m_t", "half_ratio", "h", "centred", "h_t",
         ):
             full[name] = keep.tile([P, H], F32, name=name)
         stats = keep.tile([P, BLOCKS_PER_GATE, 6], F32, name="stats")
         function_of = {"f": ACT.Tanh, "i": ACT.Exp, "z": ACT.Tanh, "o": ACT.Tanh}
         scale_of = {"f": 0.5, "i": 1.0, "z": 1.0, "o": 0.5}
-        result_of = {"f": "tanh_f", "i": "i", "z": "z", "o": "tanh_o"}
+        sums = {}
+        biased = {}
 
-        def gate_and_columns(block):
-            gate, j = divmod(block, BLOCKS_PER_GATE)
-            return GATES[gate], j, slice(j * P, (j + 1) * P)
+        def columns(block):
+            return slice(0, H) if block is None else slice(block * P, (block + 1) * P)
 
-        def add_bias(block):
-            gate, j, cols = gate_and_columns(block)
-            biased[block] = small_pool.tile([P, P], F32, name="biased")
-            nc.vector.tensor_add(out=biased[block][:], in0=sums[block][:], in1=spread[gate][:, cols])
+        def add_bias(gate, block):
+            cols = columns(block)
+            width = cols.stop - cols.start
+            biased[(gate, block)] = small_pool.tile([P, width], F32, name="biased")
+            nc.vector.tensor_add(
+                out=biased[(gate, block)][:], in0=sums[(gate, block)][:], in1=spread[gate][:, cols]
+            )
 
-        def apply_function(block):
-            gate, j, cols = gate_and_columns(block)
+        def apply_function(gate, block):
             nc.scalar.activation(
-                out=full[result_of[gate]][:, cols], in_=biased[block][:],
+                out=full["act_" + gate][:, columns(block)], in_=biased[(gate, block)][:],
                 func=function_of[gate], scale=scale_of[gate],
             )
 
-        def combine(block):
-            gate, j, cols = gate_and_columns(block)
-            if gate == "f":
-                for name in previous:
-                    nc.vector.scalar_tensor_tensor(
-                        out=full["f_" + name][:, cols], in0=full["tanh_f"][:, cols], scalar=1.0,
-                        in1=half_previous[name][:, cols], op0=ALU.add, op1=ALU.mult,
-                    )
-            if gate == "i":
-                nc.vector.scalar_tensor_tensor(
-                    out=full["denominator"][:, cols], in0=full["i"][:, cols], scalar=DIV_EPS,
-                    in1=full["f_n"][:, cols], op0=ALU.add, op1=ALU.add,
-                )
-                nc.vector.tensor_add(
-                    out=full["n_t"][:, cols], in0=full["f_n"][:, cols], in1=full["i"][:, cols]
-                )
-                nc.vector.reciprocal(out=full["reciprocal"][:, cols], in_=full["denominator"][:, cols])
-            if gate == "z":
-                nc.vector.tensor_mul(
-                    out=full["i_z"][:, cols], in0=full["i"][:, cols], in1=full["z"][:, cols]
-                )
-                nc.vector.tensor_max(
-                    out=full["larger"][:, cols], in0=full["f_m"][:, cols], in1=full["i_z"][:, cols]
-                )
-                nc.vector.tensor_add(
-                    out=full["c_t"][:, cols], in0=full["f_c"][:, cols], in1=full["i_z"][:, cols]
-                )
-                nc.vector.scalar_tensor_tensor(
-                    out=full["m_t"][:, cols], in0=full["i_z"][:, cols], scalar=-1.0,
-                    in1=full["larger"][:, cols], op0=ALU.mult, op1=ALU.max,
-                )
-                nc.vector.scalar_tensor_tensor(
-                    out=full["half_ratio"][:, cols], in0=full["c_t"][:, cols], scalar=0.5,
-                    in1=full["reciprocal"][:, cols], op0=ALU.mult, op1=ALU.mult,
-                )
-                if j == BLOCKS_PER_GATE - 1:
-                    nc.sync.dma_start(out=out_1, in_=full["c_t"][:])
-                    nc.sync.dma_start(out=out_2, in_=full["n_t"][:])
-                    nc.sync.dma_start(out=out_3, in_=full["m_t"][:])
-            if gate == "o":
-                nc.vector.scalar_tensor_tensor(
-                    out=full["h"][:, cols], in0=full["tanh_o"][:, cols], scalar=1.0,
-                    in1=full["half_ratio"][:, cols], op0=ALU.add, op1=ALU.mult,
-                )
-                nc.vector.bn_stats(out=stats[:, j, :], in_=full["h"][:, cols])
+        def stt(out, in0, scalar, in1, op0, op1, cols=slice(0, H)):
+            nc.vector.scalar_tensor_tensor(
+                out=full[out][:, cols], in0=full[in0][:, cols], scalar=scalar, in1=in1, op0=op0, op1=op1
+            )
 
+        def forget(name):
+            stt("f_" + name, "act_f", 1.0, half_previous[name][:], ALU.add, ALU.mult)
 
-        units = [[t] for t in range(len(pieces)) if pieces[t][0] < BLOCKS - 1]
-        units.append([t for t in range(len(pieces)) if pieces[t][0] == BLOCKS - 1])
+        def new_n():
+            nc.vector.tensor_add(out=full["n_t"][:], in0=full["f_n"][:], in1=full["act_i"][:])
+            nc.gpsimd.dma_start(out=out_2, in_=full["n_t"][:])
 
-        def unit(number):
-            return units[number] if 0 <= number < len(units) else []
+        def denominator():
+            stt("denominator", "act_i", DIV_EPS, full["f_n"][:], ALU.add, ALU.add)
 
-        def finished_block(number):
-            for t in unit(number):
-                if pieces[t][1] + pieces[t][2] == PASSES:
-                    return pieces[t][0]
-            return None
+        def reciprocal(block):
+            cols = columns(block)
+            nc.vector.reciprocal(out=full["reciprocal"][:, cols], in_=full["denominator"][:, cols])
 
+        def i_z():
+            nc.vector.tensor_mul(out=full["i_z"][:], in0=full["act_i"][:], in1=full["act_z"][:])
+
+        def new_c():
+            nc.vector.tensor_add(out=full["c_t"][:], in0=full["f_c"][:], in1=full["i_z"][:])
+            nc.gpsimd.dma_start(out=out_1, in_=full["c_t"][:])
+
+        def larger():
+            nc.vector.tensor_max(out=full["larger"][:], in0=full["f_m"][:], in1=full["i_z"][:])
+
+        def new_m():
+            stt("m_t", "i_z", -1.0, full["larger"][:], ALU.mult, ALU.max)
+            nc.gpsimd.dma_start(out=out_3, in_=full["m_t"][:])
+
+        def half_ratio():
+            stt("half_ratio", "c_t", 0.5, full["reciprocal"][:], ALU.mult, ALU.mult)
+
+        def hidden(block):
+            cols = columns(block)
+            stt("h", "act_o", 1.0, full["half_ratio"][:, cols], ALU.add, ALU.mult, cols)
+
+        def statistics(block):
+            nc.vector.bn_stats(out=stats[:, block, :], in_=full["h"][:, columns(block)])
+
+        later = {
+            "f": [lambda: forget("n"), lambda: forget("c"), lambda: forget("m")],
+            "i": [denominator, new_n] + [lambda block=block: reciprocal(block) for block in range(BLOCKS_PER_GATE)],
+            "z": [i_z, larger, new_c, new_m, half_ratio],
+        }
+        waiting = []
+
+        loaded = RAW_BUFS - len(X_PARTS)
+        served = 0
         grouped_of = {}
         codes_of = {}
         scales_of = {}
-        sums = {}
-        biased = {}
-        for step in range(len(units) + MULTIPLY_LAG + 2):
-            left_for_vector = None
-            for t in unit(step):
-                block, first_pass, n_passes = pieces[t]
-                if t + PREFETCH < len(pieces):
-                    load_weight_piece(t + PREFETCH)
-                grouped_of[t], left = transpose_piece(block, first_pass, n_passes)
-                if left is not None:
-                    left_for_vector = left
 
-            for t in unit(step - 1):
-                n_words = pieces[t][2] * P
-                codes_of[t] = quantised_pool.tile([P, n_words], U32, name="w_codes", align_bytes=64)
-                scales_of[t] = quantised_pool.tile([P, n_words], U8, name="w_scales", align_bytes=64)
-                quantise_piece(grouped_of[t], codes_of[t][:], scales_of[t][:])
+        def finished(t):
+            if 0 <= t < len(steps) and steps[t]["first"] + steps[t]["passes"] == PASSES:
+                return steps[t]["gate"], steps[t]["block"]
+            return None
 
-            if step == MULTIPLY_LAG:
-                spread_row_vectors()
-
-            for t in unit(step - MULTIPLY_LAG):
-                block, first_pass, n_passes = pieces[t]
-                if first_pass == 0:
-                    sums[block] = sum_pool.tile([P, P], F32, name="sums")
-                for q in range(n_passes):
-                    x_words = slice((first_pass + q) * P, (first_pass + q + 1) * P)
-                    w_words = slice(q * P, (q + 1) * P)
-                    nc.tensor.matmul_mx(
-                        out=sums[block][:],
-                        lhsT=x_codes[:, x_words].bitcast(FP8X4),
-                        lhsT_scale=x_scales[:, x_words],
-                        rhs=codes_of[t][:, w_words].bitcast(FP8X4),
-                        rhs_scale=scales_of[t][:, w_words],
-                        start=(first_pass + q == 0),
-                        stop=(first_pass + q == PASSES - 1),
+        for t in range(len(steps) + MULTIPLY_LAG + 3):
+            if t < len(steps):
+                step = steps[t]
+                first_load = min(number for number, column in step["units"])
+                while loaded < first_load + RAW_BUFS and loaded < len(loads):
+                    load(loaded)
+                    loaded += 1
+                sources = []
+                for number, column in step["units"]:
+                    sources.append(
+                        places_of.get((t, number), {}).get(column, (raw_of[number], column, None))
                     )
-
-            if finished_block(step - MULTIPLY_LAG - 1) is not None:
-                add_bias(finished_block(step - MULTIPLY_LAG - 1))
-                apply_function(finished_block(step - MULTIPLY_LAG - 1))
-            if finished_block(step - MULTIPLY_LAG - 2) is not None:
-                combine(finished_block(step - MULTIPLY_LAG - 2))
-            vector_empties(left_for_vector)
+                grouped_of[t] = transpose_units(sources)
+            sort_step(t + 1)
+            if 0 <= t - 1 < len(steps):
+                n_words = len(steps[t - 1]["units"]) * P
+                codes_of[t - 1] = quantised_pool.tile([P, n_words], U32, name="w_codes", align_bytes=64)
+                scales_of[t - 1] = quantised_pool.tile([P, n_words], U8, name="w_scales", align_bytes=64)
+                quantise(grouped_of[t - 1], codes_of[t - 1][:], scales_of[t - 1][:])
+            if t == 5:
+                spread_row_vectors()
+            m = t - MULTIPLY_LAG
+            if 0 <= m < len(steps):
+                step = steps[m]
+                key = (step["gate"], step["block"])
+                width = H if step["block"] is None else P
+                if step["first"] == 0:
+                    sums[key] = sum_pool.tile([P, width], F32, name="sums")
+                for g in range(step["passes"]):
+                    q = step["first"] + g
+                    nc.tensor.matmul_mx(
+                        out=sums[key][:],
+                        lhsT=x_codes[:, q * P : (q + 1) * P].bitcast(FP8X4),
+                        lhsT_scale=x_scales[:, q * P : (q + 1) * P],
+                        rhs=codes_of[m][:, g * width : (g + 1) * width].bitcast(FP8X4),
+                        rhs_scale=scales_of[m][:, g * width : (g + 1) * width],
+                        start=(q == 0),
+                        stop=(q == PASSES - 1),
+                    )
+            done = finished(m - 1)
+            if done is not None:
+                add_bias(done[0], done[1])
+                apply_function(done[0], done[1])
+            done = finished(m - 2)
+            if done is not None and done[1] is None:
+                waiting.extend(later[done[0]])
+            for turn in range(2 if len(waiting) - served > 2 else 1):
+                if served < len(waiting):
+                    waiting[served]()
+                    served += 1
+            if done is not None and done[1] is not None:
+                hidden(done[1])
+                statistics(done[1])
 
         mean_var = keep.tile([P, 2], F32, name="mean_var")
         nc.vector.bn_aggr(out=mean_var[:], in_=stats[:].rearrange("p j s -> p (j s)"))
@@ -325,8 +397,10 @@ def tile_slstmcell_k_kernel(
             out=full["centred"][:], in0=full["h"][:], scalar=mean_var[:, 0:1],
             in1=spread["gamma"], op0=ALU.subtract, op1=ALU.mult,
         )
-        nc.vector.scalar_tensor_tensor(
-            out=full["h_t"][:], in0=full["centred"][:], scalar=inv_std[:],
-            in1=spread["beta"], op0=ALU.mult, op1=ALU.add,
-        )
-        nc.sync.dma_start(out=out_0, in_=full["h_t"][:])
+        for part, queue in enumerate((nc.sync, nc.scalar)):
+            cols = slice(part * H // 2, (part + 1) * H // 2)
+            nc.vector.scalar_tensor_tensor(
+                out=full["h_t"][:, cols], in0=full["centred"][:, cols], scalar=inv_std[:],
+                in1=spread["beta"][:, cols], op0=ALU.mult, op1=ALU.add,
+            )
+            queue.dma_start(out=out_0[:, cols], in_=full["h_t"][:, cols])

@@ -155,17 +155,18 @@ def tile_slstmcell_k_kernel(
             )
 
         def sort_words(raw, n_rows, first, n, pitch):
-            half = n_rows * n * P
-            out_tile = sorted_pool.tile([P, 2 * half], F32, name="sorted")
-            in_ = raw[:].bitcast(F32).rearrange("p (r n u) -> p u r n", r=n_rows, u=2)
-            in_ = in_[:, :, :, first * P : (first + n) * P]
-            nc.vector.tensor_copy(
-                out=out_tile[:].rearrange("p (u r n) -> p u r n", u=2, r=n_rows), in_=in_
-            )
+            out_tile = sorted_pool.tile([P, n_rows * n * PASS_PAIRS], F32, name="sorted")
+            in_ = raw[:].bitcast(F32).rearrange("p (r g w) -> p r g w", r=n_rows, w=PASS_PAIRS)
+            in_ = in_[:, :, first : first + n, :].rearrange("p r g (n u) -> p r g u n", u=2)
+            out = out_tile[:].rearrange("p (r g u n) -> p r g u n", r=n_rows, g=n, u=2)
+            if n_rows == 1:
+                in_ = in_[:, 0, :, :, :]
+                out = out[:, 0, :, :, :]
+            nc.vector.tensor_copy(out=out, in_=in_)
             places = {}
             for r in range(n_rows):
                 for g in range(n):
-                    places[(r * pitch + first + g) * PASS_PAIRS] = (out_tile, (r * n + g) * P, half)
+                    places[(r * pitch + first + g) * PASS_PAIRS] = (out_tile, (r * n + g) * PASS_PAIRS, P)
             return places
 
         def transpose_units(sources):

@@ -30,12 +30,11 @@ WIDE_GATES = ("f", "i", "z")
 NARROW_GATE = "o"
 WIDE_LOAD_PASSES = 4
 WIDE_STEP_PASSES = 2
-NARROW_STEP_PASSES = 8
-WIDE_SPLIT = (1,)
-NARROW_SORTED = 4
+TILE_PASSES = 16
+BLOCK = 32
 
 TRANSPOSE_BANKS = 6
-RAW_BUFS = 10
+RAW_BUFS = 6
 X_PARTS = (2, 4, 6, 4)
 MULTIPLY_LAG = 2
 
@@ -62,69 +61,61 @@ def tile_slstmcell_k_kernel(
         bank_pool = ctx.enter_context(tc.psum_pool(name="banks", bufs=TRANSPOSE_BANKS))
         sum_pool = ctx.enter_context(tc.psum_pool(name="sums", bufs=2))
 
-        loads = []
+        tiles = []
         steps = []
         for gate in WIDE_GATES:
             for first in range(0, PASSES, WIDE_LOAD_PASSES):
                 k_range = slice(first * K_PASS, (first + WIDE_LOAD_PASSES) * K_PASS)
-                base = len(loads)
+                half = 2 * WIDE_LOAD_PASSES * K_PASS
+                pieces = []
                 for pair in range(2):
                     rows = slice(pair * 2 * P, (pair + 1) * 2 * P)
-                    loads.append((2 * WIDE_LOAD_PASSES * K_PASS, weights[gate][rows, k_range], 2))
-                for sub in range(WIDE_LOAD_PASSES // WIDE_STEP_PASSES):
-                    n_sorted = WIDE_SPLIT[len(steps) % len(WIDE_SPLIT)]
-                    units = []
-                    for g in range(WIDE_STEP_PASSES):
-                        for r in range(BLOCKS_PER_GATE):
-                            pass_in_load = sub * WIDE_STEP_PASSES + g
-                            units.append((base + r // 2, ((r % 2) * WIDE_LOAD_PASSES + pass_in_load) * PASS_PAIRS))
+                    pieces.append((pair * half, half, weights[gate][rows, k_range], 2))
+                for sub in range(0, WIDE_LOAD_PASSES, WIDE_STEP_PASSES):
                     steps.append({
-                        "gate": gate, "block": None, "first": first + sub * WIDE_STEP_PASSES,
-                        "passes": WIDE_STEP_PASSES, "units": units,
-                        "sort": [(base + q, 2, sub * WIDE_STEP_PASSES, WIDE_STEP_PASSES, WIDE_LOAD_PASSES) for q in range(n_sorted)],
+                        "gate": gate, "block": None, "first": first + sub, "passes": WIDE_STEP_PASSES,
+                        "tile": len(tiles), "rows": BLOCKS_PER_GATE, "column": sub,
                     })
+                tiles.append((BLOCKS_PER_GATE, pieces))
         for block in range(BLOCKS_PER_GATE):
-            last = block == BLOCKS_PER_GATE - 1
+            rows = slice(block * P, (block + 1) * P)
             first = 0
-            for n in (8, 4, 2, 2) if last else (8, 8):
-                rows = slice(block * P, (block + 1) * P)
+            pieces = []
+            for n in (8, 4, 2, 2) if block == BLOCKS_PER_GATE - 1 else (8, 8):
                 k_range = slice(first * K_PASS, (first + n) * K_PASS)
-                n_sorted = n * NARROW_SORTED // NARROW_STEP_PASSES if n == NARROW_STEP_PASSES else 0
+                pieces.append((first * K_PASS, n * K_PASS, weights[NARROW_GATE][rows, k_range], 1))
                 steps.append({
                     "gate": NARROW_GATE, "block": block, "first": first, "passes": n,
-                    "units": [(len(loads), g * PASS_PAIRS) for g in range(n)],
-                    "sort": [(len(loads), 1, 0, n_sorted, n)] if n_sorted else [],
+                    "tile": len(tiles), "rows": 1, "column": first,
                 })
-                loads.append((n * K_PASS, weights[NARROW_GATE][rows, k_range], 1))
                 first += n
+            tiles.append((1, pieces))
 
         raw_of = {}
 
-        def load(t):
-            if t < len(loads):
-                width, source, n_rows = loads[t]
-                raw = raw_pool.tile([P, width], BF16, name="raw")
-                raw_of[t] = raw
-                if n_rows == 1:
-                    nc.sync.dma_start(out=raw[:], in_=source)
+        def load(number):
+            n_rows, pieces = tiles[number]
+            raw = raw_pool.tile([P, TILE_PASSES * K_PASS], BF16, name="raw")
+            raw_of[number] = raw
+            for column, width, source, n in pieces:
+                place = raw[:, column : column + width]
+                if n == 1:
+                    nc.sync.dma_start(out=place, in_=source)
                 else:
                     nc.sync.dma_start(
-                        out=raw[:].rearrange("p (r k) -> p r k", r=n_rows),
-                        in_=source.rearrange("(r p) k -> p r k", r=n_rows),
+                        out=place.rearrange("p (r k) -> p r k", r=n),
+                        in_=source.rearrange("(r p) k -> p r k", r=n),
                     )
 
-        x_raw = []
+        x_raw = raw_pool.tile([P, TILE_PASSES * K_PASS], BF16, name="raw")
         first = 0
         for n in X_PARTS:
-            raw = raw_pool.tile([P, n * K_PASS], BF16, name="raw")
             k0 = first * K_PASS
             k1 = min((first + n) * K_PASS, IN)
-            nc.sync.dma_start(out=raw[:, 0 : k1 - k0], in_=x[:, k0:k1])
-            if k1 == IN:
-                nc.sync.dma_start(out=raw[:, k1 - k0 : n * K_PASS], in_=h_prev)
-            x_raw.append((raw, first, n))
+            nc.sync.dma_start(out=x_raw[:, k0:k1], in_=x[:, k0:k1])
             first += n
-        for number in range(RAW_BUFS - len(X_PARTS)):
+        nc.sync.dma_start(out=x_raw[:, IN:D], in_=h_prev)
+        for number in range(RAW_BUFS - 1):
             load(number)
 
         identity = keep.tile([P, P], F32, name="identity")
@@ -154,19 +145,25 @@ def tile_slstmcell_k_kernel(
                 scalar1=0.5, scalar2=0.0, op0=ALU.mult, op1=ALU.add,
             )
 
-        def sort_words(raw, n_rows, first, n, pitch):
-            out_tile = sorted_pool.tile([P, n_rows * n * PASS_PAIRS], F32, name="sorted")
-            in_ = raw[:].bitcast(F32).rearrange("p (r g w) -> p r g w", r=n_rows, w=PASS_PAIRS)
-            in_ = in_[:, :, first : first + n, :].rearrange("p r g (n u) -> p r g u n", u=2)
-            out = out_tile[:].rearrange("p (r g u n) -> p r g u n", r=n_rows, g=n, u=2)
+        def sort_passes(raw, n_rows, column, first, n):
+            n_pairs = n // 2
+            pitch = TILE_PASSES // n_rows
+            out_tile = sorted_pool.tile([P, n_rows * n_pairs * K_PASS], BF16, name="sorted")
+            in_ = raw[:].rearrange("p (r g j k) -> p r g j k", r=n_rows, j=2, k=K_PASS)
+            in_ = in_[:, :, column // 2 : column // 2 + n_pairs, 0, :]
+            out = out_tile[:].rearrange("p (r g k) -> p r g k", r=n_rows, g=n_pairs)
             if n_rows == 1:
-                in_ = in_[:, 0, :, :, :]
-                out = out[:, 0, :, :, :]
-            nc.vector.tensor_copy(out=out, in_=in_)
+                in_, out = in_[:, 0, :, :], out[:, 0, :, :]
+            else:
+                in_, out = in_[:, :, 0, :], out[:, :, 0, :]
+            nc.vector.tensor_copy(
+                out=out.rearrange("p g (u b e) -> p g u b e", u=2, e=BLOCK // 2),
+                in_=in_.rearrange("p g (b u e) -> p g u b e", u=2, e=BLOCK // 2),
+            )
             places = {}
             for r in range(n_rows):
-                for g in range(n):
-                    places[(r * pitch + first + g) * PASS_PAIRS] = (out_tile, (r * n + g) * PASS_PAIRS, P)
+                for g in range(n_pairs):
+                    places[r * pitch + column + 2 * g] = (out_tile, (r * n_pairs + g) * PASS_PAIRS, True)
             return places
 
         def transpose_units(sources):
@@ -175,12 +172,13 @@ def tile_slstmcell_k_kernel(
             for b in range(len(sources) // UNITS_PER_BANK):
                 bank = bank_pool.tile([P, 2, UNITS_PER_BANK * P], F32, name="bank")
                 for s in range(UNITS_PER_BANK):
-                    tile, column, half = sources[b * UNITS_PER_BANK + s]
+                    tile, column, in_order = sources[b * UNITS_PER_BANK + s]
+                    words_of = tile[:].bitcast(F32)
                     for u in range(2):
-                        if half is None:
-                            words = tile[:].bitcast(F32)[:, column + u : column + PASS_PAIRS : 2]
+                        if in_order:
+                            words = words_of[:, column + u * P : column + (u + 1) * P]
                         else:
-                            words = tile[:, u * half + column : u * half + column + P]
+                            words = words_of[:, column + u : column + PASS_PAIRS : 2]
                         nc.tensor.transpose(bank[:, u, s * P : (s + 1) * P], words, identity[:])
                 span = UNITS_PER_BANK * PASS_PAIRS
                 nc.scalar.copy(
@@ -196,8 +194,19 @@ def tile_slstmcell_k_kernel(
 
         def sort_step(t):
             if t < len(steps):
-                for number, n_rows, first, n, pitch in steps[t]["sort"]:
-                    places_of[(t, number)] = sort_words(raw_of[number], n_rows, first, n, pitch)
+                step = steps[t]
+                places_of[t] = sort_passes(
+                    raw_of[step["tile"]], step["rows"], step["column"], step["first"], step["passes"]
+                )
+
+        def sources_of(raw, places, n_rows, column, n):
+            pitch = TILE_PASSES // n_rows
+            units = []
+            for g in range(n):
+                for r in range(n_rows):
+                    place = r * pitch + column + g
+                    units.append(places.get(place, (raw, place * PASS_PAIRS, False)))
+            return units
 
         x_codes = keep.tile([P, PASSES * P], U32, name="x_codes", align_bytes=64)
         x_scales = keep.tile([P, PASSES * P], U8, name="x_scales", align_bytes=64)
@@ -213,20 +222,20 @@ def tile_slstmcell_k_kernel(
                 )
                 a += size
 
-        places = {}
-        grouped_before = None
-        for part, (raw, first, n) in enumerate(x_raw):
-            grouped = transpose_units(
-                [places.get(g * PASS_PAIRS, (raw, g * PASS_PAIRS, None)) for g in range(n)]
-            )
-            if part + 1 < len(x_raw):
-                places = sort_words(x_raw[part + 1][0], 1, 0, x_raw[part + 1][2], x_raw[part + 1][2])
+        first = 0
+        before = None
+        places = sort_passes(x_raw, 1, 0, 0, X_PARTS[0])
+        for part, n in enumerate(X_PARTS):
+            grouped = transpose_units(sources_of(x_raw, places, 1, first, n))
+            if part + 1 < len(X_PARTS):
+                places = sort_passes(x_raw, 1, first + n, first + n, X_PARTS[part + 1])
             else:
                 sort_step(0)
-            if grouped_before is not None:
-                quantise_x(grouped_before, x_raw[part - 1][1], x_raw[part - 1][2])
-            grouped_before = grouped
-        quantise_x(grouped_before, x_raw[-1][1], x_raw[-1][2])
+            if before is not None:
+                quantise_x(before[0], before[1], before[2])
+            before = (grouped, first, n)
+            first += n
+        quantise_x(before[0], before[1], before[2])
 
         spread = {}
 
@@ -323,7 +332,7 @@ def tile_slstmcell_k_kernel(
         }
         waiting = []
 
-        loaded = RAW_BUFS - len(X_PARTS)
+        loaded = RAW_BUFS - 1
         served = 0
         grouped_of = {}
         codes_of = {}
@@ -337,19 +346,15 @@ def tile_slstmcell_k_kernel(
         for t in range(len(steps) + MULTIPLY_LAG + 3):
             if t < len(steps):
                 step = steps[t]
-                first_load = min(number for number, column in step["units"])
-                while loaded < first_load + RAW_BUFS and loaded < len(loads):
+                while loaded < step["tile"] + RAW_BUFS and loaded < len(tiles):
                     load(loaded)
                     loaded += 1
-                sources = []
-                for number, column in step["units"]:
-                    sources.append(
-                        places_of.get((t, number), {}).get(column, (raw_of[number], column, None))
-                    )
-                grouped_of[t] = transpose_units(sources)
+                grouped_of[t] = transpose_units(
+                    sources_of(raw_of[step["tile"]], places_of[t], step["rows"], step["column"], step["passes"])
+                )
             sort_step(t + 1)
             if 0 <= t - 1 < len(steps):
-                n_words = len(steps[t - 1]["units"]) * P
+                n_words = steps[t - 1]["rows"] * steps[t - 1]["passes"] * P
                 codes_of[t - 1] = quantised_pool.tile([P, n_words], U32, name="w_codes", align_bytes=64)
                 scales_of[t - 1] = quantised_pool.tile([P, n_words], U8, name="w_scales", align_bytes=64)
                 quantise(grouped_of[t - 1], codes_of[t - 1][:], scales_of[t - 1][:])

@@ -22,21 +22,31 @@ DIV_EPS = 1e-6
 PACK = 4
 K_PASS = P * PACK
 PASSES = D // K_PASS
-PASS_PAIRS = K_PASS // 2
+PASS_WORDS = K_PASS // 2
+BLOCK = 32
 BLOCKS_PER_GATE = H // P
 UNITS_PER_BANK = 2
 
+GROUP = 4
+SORTED = (2, 2, 1, 1)
 WIDE_GATES = ("f", "i", "z")
 NARROW_GATE = "o"
-WIDE_LOAD_PASSES = 4
-WIDE_STEP_PASSES = 2
-TILE_PASSES = 16
-BLOCK = 32
-
+X_LOADS = (2, 2, 4, 8)
+X_STEPS = (4, 4, 4, 4)
+VECTOR_BANK_STEPS = 6
+TAPER = (8, 4, 4)
+RAW_BUFS = 5
 TRANSPOSE_BANKS = 6
-RAW_BUFS = 6
-X_PARTS = (2, 4, 6, 4)
-MULTIPLY_LAG = 2
+QUANTISE_LAG = 2
+MULTIPLY_LAG = 3
+MULTIPLY_RUN = 2
+SPREAD_STEPS = (8, 9, 10)
+VECTOR_BANK = 3
+EARLY_STEPS = 18
+EARLY_BANK_STEPS = 2
+EARLY_TILES = 0
+SORT_AHEAD = 2
+SORT_FIRST = False
 
 FLOPS = 2 * P * D * 4 * H
 
@@ -54,81 +64,87 @@ def tile_slstmcell_k_kernel(
         ctx.enter_context(tc.manual_schedule())
         keep = ctx.enter_context(tc.tile_pool(name="keep", bufs=1))
         raw_pool = ctx.enter_context(tc.tile_pool(name="raw", bufs=RAW_BUFS))
-        sorted_pool = ctx.enter_context(tc.tile_pool(name="sorted", bufs=4))
+        sorted_pool = ctx.enter_context(tc.tile_pool(name="sorted", bufs=3))
         grouped_pool = ctx.enter_context(tc.tile_pool(name="grouped", bufs=4))
-        quantised_pool = ctx.enter_context(tc.tile_pool(name="quantised", bufs=3))
+        quantised_pool = ctx.enter_context(tc.tile_pool(name="quantised", bufs=4))
         small_pool = ctx.enter_context(tc.tile_pool(name="small", bufs=2))
         bank_pool = ctx.enter_context(tc.psum_pool(name="banks", bufs=TRANSPOSE_BANKS))
         sum_pool = ctx.enter_context(tc.psum_pool(name="sums", bufs=2))
 
         tiles = []
+        sorts = []
         steps = []
+
+        def add_step(gate, block, columns, first, sort):
+            steps.append({
+                "gate": gate, "block": block, "tile": len(tiles), "columns": columns,
+                "passes": [first + c for c in columns], "sort": sort,
+            })
+
+        pieces = []
+        first = 0
+        for n in X_LOADS:
+            k0, k1 = first * K_PASS, min((first + n) * K_PASS, IN)
+            pieces.append((k0, x[:, k0:k1]))
+            first += n
+        pieces.append((IN, h_prev))
+        first = 0
+        for n in X_STEPS:
+            add_step("x", None, list(range(first, first + n)), 0, len(sorts))
+            sorts.append((0, first, n, SORTED[first // GROUP]))
+            first += n
+        tiles.append((1, PASSES, pieces))
+        half = GROUP // 2
         for gate in WIDE_GATES:
-            for first in range(0, PASSES, WIDE_LOAD_PASSES):
-                k_range = slice(first * K_PASS, (first + WIDE_LOAD_PASSES) * K_PASS)
-                half = 2 * WIDE_LOAD_PASSES * K_PASS
+            for first in range(0, PASSES, GROUP):
                 pieces = []
-                for pair in range(2):
-                    rows = slice(pair * 2 * P, (pair + 1) * 2 * P)
-                    pieces.append((pair * half, half, weights[gate][rows, k_range], 2))
-                for sub in range(0, WIDE_LOAD_PASSES, WIDE_STEP_PASSES):
-                    steps.append({
-                        "gate": gate, "block": None, "first": first + sub, "passes": WIDE_STEP_PASSES,
-                        "tile": len(tiles), "rows": BLOCKS_PER_GATE, "column": sub,
-                    })
-                tiles.append((BLOCKS_PER_GATE, pieces))
+                early = len(tiles) <= EARLY_TILES
+                for a, b in ((half, GROUP), (0, half)) if early else ((0, GROUP),):
+                    for r in range(0, BLOCKS_PER_GATE, 2):
+                        source = weights[gate][
+                            r * P : (r + 2) * P, (first + a) * K_PASS : (first + b) * K_PASS
+                        ]
+                        pieces.append(((r * GROUP + a) * K_PASS, source))
+                for columns in ([2, 3], [0, 1]) if early else ([0, 2], [1, 3]):
+                    add_step(gate, None, columns, first, len(sorts))
+                sorts.append((len(tiles), 0, GROUP, SORTED[first // GROUP]))
+                tiles.append((BLOCKS_PER_GATE, GROUP, pieces))
         for block in range(BLOCKS_PER_GATE):
             rows = slice(block * P, (block + 1) * P)
-            first = 0
             pieces = []
-            for n in (8, 4, 2, 2) if block == BLOCKS_PER_GATE - 1 else (8, 8):
-                k_range = slice(first * K_PASS, (first + n) * K_PASS)
-                pieces.append((first * K_PASS, n * K_PASS, weights[NARROW_GATE][rows, k_range], 1))
-                steps.append({
-                    "gate": NARROW_GATE, "block": block, "first": first, "passes": n,
-                    "tile": len(tiles), "rows": 1, "column": first,
-                })
+            first = 0
+            for n in TAPER if block == BLOCKS_PER_GATE - 1 else (8, 8):
+                pieces.append((first * K_PASS, weights[NARROW_GATE][rows, first * K_PASS : (first + n) * K_PASS]))
+                add_step(NARROW_GATE, block, list(range(first, first + n)), 0, len(sorts))
+                sorts.append((len(tiles), first, n, SORTED[first // GROUP]))
                 first += n
-            tiles.append((1, pieces))
+            tiles.append((1, PASSES, pieces))
 
         raw_of = {}
+        loaded = 0
 
         def load(number):
-            n_rows, pieces = tiles[number]
-            raw = raw_pool.tile([P, TILE_PASSES * K_PASS], BF16, name="raw")
+            n_rows, n_passes, pieces = tiles[number]
+            raw = raw_pool.tile([P, n_rows * n_passes * K_PASS], BF16, name="raw")
             raw_of[number] = raw
-            for column, width, source, n in pieces:
-                place = raw[:, column : column + width]
-                if n == 1:
-                    nc.sync.dma_start(out=place, in_=source)
+            for column, source in pieces:
+                rows, width = source.shape
+                if rows == P:
+                    nc.sync.dma_start(out=raw[:, column : column + width], in_=source)
                 else:
-                    nc.sync.dma_start(
-                        out=place.rearrange("p (r k) -> p r k", r=n),
-                        in_=source.rearrange("(r p) k -> p r k", r=n),
-                    )
+                    start = column % (n_passes * K_PASS)
+                    part = column // (n_passes * K_PASS)
+                    parts = raw[:].rearrange("p (a k) -> p a k", a=n_rows)[:, part : part + 2, start : start + width]
+                    nc.sync.dma_start(out=parts, in_=source.rearrange("(a p) k -> p a k", a=2))
 
-        x_raw = raw_pool.tile([P, TILE_PASSES * K_PASS], BF16, name="raw")
-        first = 0
-        for n in X_PARTS:
-            k0 = first * K_PASS
-            k1 = min((first + n) * K_PASS, IN)
-            nc.sync.dma_start(out=x_raw[:, k0:k1], in_=x[:, k0:k1])
-            first += n
-        nc.sync.dma_start(out=x_raw[:, IN:D], in_=h_prev)
-        for number in range(RAW_BUFS - 1):
-            load(number)
-
+        load(0)
+        load(1)
+        load(2)
+        load(3)
         identity = keep.tile([P, P], F32, name="identity")
         make_identity(nc, identity[:])
-        ones = keep.tile([P, P], BF16, name="ones")
-        nc.vector.memset(ones[:], 1.0)
-        minus_half = keep.tile([P, 1], F32, name="minus_half")
-        nc.vector.memset(minus_half[:], -0.5)
         vector_rows = keep.tile([P, len(row_vectors) * H], BF16, name="vector_rows")
         nc.vector.memset(vector_rows[:].bitcast(I32), 0)
-        table_warmer = keep.tile([P, 1], F32, name="table_warmer")
-        nc.scalar.activation(out=table_warmer[:], in_=minus_half[:], func=ACT.Tanh)
-
         for v, name in enumerate(row_vectors):
             nc.gpsimd.dma_start(
                 out=vector_rows[0:1, v * H : (v + 1) * H], in_=row_vectors[name].unsqueeze(0)
@@ -137,6 +153,16 @@ def tile_slstmcell_k_kernel(
         for name in previous:
             previous_bf16[name] = keep.tile([P, H], BF16, name="previous_" + name)
             nc.gpsimd.dma_start(out=previous_bf16[name][:], in_=previous[name])
+        for number in range(4, RAW_BUFS):
+            load(number)
+        loaded = RAW_BUFS
+
+        ones = keep.tile([P, P], BF16, name="ones")
+        nc.vector.memset(ones[:], 1.0)
+        minus_half = keep.tile([P, 1], F32, name="minus_half")
+        nc.vector.memset(minus_half[:], -0.5)
+        table_warmer = keep.tile([P, 1], F32, name="table_warmer")
+        nc.scalar.activation(out=table_warmer[:], in_=minus_half[:], func=ACT.Tanh)
         half_previous = {}
         for name in previous:
             half_previous[name] = keep.tile([P, H], F32, name="half_previous_" + name)
@@ -145,131 +171,130 @@ def tile_slstmcell_k_kernel(
                 scalar1=0.5, scalar2=0.0, op0=ALU.mult, op1=ALU.add,
             )
 
-        def sort_passes(raw, n_rows, column, first, n):
-            n_pairs = n // 2
-            pitch = TILE_PASSES // n_rows
-            out_tile = sorted_pool.tile([P, n_rows * n_pairs * K_PASS], BF16, name="sorted")
-            in_ = raw[:].rearrange("p (r g j k) -> p r g j k", r=n_rows, j=2, k=K_PASS)
-            in_ = in_[:, :, column // 2 : column // 2 + n_pairs, 0, :]
-            out = out_tile[:].rearrange("p (r g k) -> p r g k", r=n_rows, g=n_pairs)
-            if n_rows == 1:
-                in_, out = in_[:, 0, :, :], out[:, 0, :, :]
-            else:
-                in_, out = in_[:, :, 0, :], out[:, :, 0, :]
-            nc.vector.tensor_copy(
-                out=out.rearrange("p g (u b e) -> p g u b e", u=2, e=BLOCK // 2),
-                in_=in_.rearrange("p g (b u e) -> p g u b e", u=2, e=BLOCK // 2),
-            )
-            places = {}
-            for r in range(n_rows):
-                for g in range(n_pairs):
-                    places[r * pitch + column + 2 * g] = (out_tile, (r * n_pairs + g) * PASS_PAIRS, True)
-            return places
+        sorted_of = {}
 
-        def transpose_units(sources):
-            grouped = grouped_pool.tile([P, len(sources) * K_PASS], BF16, name="grouped", align_bytes=64)
-            grouped_words = grouped[:].bitcast(F32)
-            for b in range(len(sources) // UNITS_PER_BANK):
+        def sort(s):
+            number, column, n, n_sorted = sorts[s]
+            n_rows, n_passes, pieces = tiles[number]
+            n_groups = n // GROUP
+            outer = n_rows * n_groups
+            size = n_sorted * K_PASS
+            out = sorted_pool.tile([P, outer * size], BF16, name="sorted")
+            in_ = raw_of[number][:].rearrange("p (a k) -> p a k", k=GROUP * K_PASS)
+            if n_rows == 1:
+                in_ = in_[:, column // GROUP : column // GROUP + n_groups, :]
+            in_ = in_[:, :, 0:size]
+            nc.vector.tensor_copy(
+                out=out[:].rearrange("p (a u b e) -> p a u b e", a=outer, u=2, e=BLOCK // 2),
+                in_=in_.rearrange("p a (b u e) -> p a u b e", u=2, e=BLOCK // 2),
+            )
+            sorted_of[s] = out
+
+        def words_of(step, c, r, u):
+            n_rows, n_passes, pieces = tiles[step["tile"]]
+            number, start, n, n_sorted = sorts[step["sort"]]
+            if c % GROUP < n_sorted:
+                part = r if n_rows > 1 else (c - start) // GROUP
+                column = part * n_sorted * PASS_WORDS + u * n_sorted * P + c % GROUP * P
+                return sorted_of[step["sort"]][:].bitcast(F32)[:, column : column + P]
+            column = (r * n_passes + c) * PASS_WORDS
+            return raw_of[step["tile"]][:].bitcast(F32)[:, column + u : column + PASS_WORDS : 2]
+
+        grouped_of = {}
+        left_for_vector = []
+
+        def transpose(t):
+            step = steps[t]
+            n_rows = tiles[step["tile"]][0]
+            units = [(c, r) for c in step["columns"] for r in range(n_rows)]
+            grouped = grouped_pool.tile([P, len(units) * K_PASS], BF16, name="grouped", align_bytes=64)
+            grouped_of[t] = grouped
+            span = UNITS_PER_BANK * PASS_WORDS
+            for b in range(len(units) // UNITS_PER_BANK):
                 bank = bank_pool.tile([P, 2, UNITS_PER_BANK * P], F32, name="bank")
                 for s in range(UNITS_PER_BANK):
-                    tile, column, in_order = sources[b * UNITS_PER_BANK + s]
-                    words_of = tile[:].bitcast(F32)
+                    c, r = units[b * UNITS_PER_BANK + s]
                     for u in range(2):
-                        if in_order:
-                            words = words_of[:, column + u * P : column + (u + 1) * P]
-                        else:
-                            words = words_of[:, column + u : column + PASS_PAIRS : 2]
-                        nc.tensor.transpose(bank[:, u, s * P : (s + 1) * P], words, identity[:])
-                span = UNITS_PER_BANK * PASS_PAIRS
-                nc.scalar.copy(
-                    out=grouped_words[:, b * span : (b + 1) * span].rearrange("p (c u) -> p c u", u=2),
-                    in_=bank[:].rearrange("p u c -> p c u"),
-                )
-            return grouped
-
-        def quantise(grouped, codes, scales):
-            nc.vector.quantize_mx(out=codes.bitcast(FP8X4), scales=scales, in_=grouped[:])
-
-        places_of = {}
-
-        def sort_step(t):
-            if t < len(steps):
-                step = steps[t]
-                places_of[t] = sort_passes(
-                    raw_of[step["tile"]], step["rows"], step["column"], step["first"], step["passes"]
-                )
-
-        def sources_of(raw, places, n_rows, column, n):
-            pitch = TILE_PASSES // n_rows
-            units = []
-            for g in range(n):
-                for r in range(n_rows):
-                    place = r * pitch + column + g
-                    units.append(places.get(place, (raw, place * PASS_PAIRS, False)))
-            return units
+                        nc.tensor.transpose(bank[:, u, s * P : (s + 1) * P], words_of(step, c, r, u), identity[:])
+                out = grouped[:].bitcast(F32)[:, b * span : (b + 1) * span].rearrange("p (c u) -> p c u", u=2)
+                in_ = bank[:].rearrange("p u c -> p c u")
+                every = EARLY_BANK_STEPS if t < EARLY_STEPS else VECTOR_BANK_STEPS
+                if t % every == every - 1 and b == VECTOR_BANK:
+                    left_for_vector.append((out, in_))
+                else:
+                    nc.scalar.copy(out=out, in_=in_)
 
         x_codes = keep.tile([P, PASSES * P], U32, name="x_codes", align_bytes=64)
         x_scales = keep.tile([P, PASSES * P], U8, name="x_scales", align_bytes=64)
+        codes_of = {}
+        scales_of = {}
 
-        def quantise_x(grouped, first, n):
-            a = 0
-            while a < n:
-                size = 4 if n - a >= 4 else 2
-                words = slice((first + a) * P, (first + a + size) * P)
-                nc.vector.quantize_mx(
-                    out=x_codes[:, words].bitcast(FP8X4), scales=x_scales[:, words],
-                    in_=grouped[:, a * K_PASS : (a + size) * K_PASS],
-                )
-                a += size
-
-        first = 0
-        before = None
-        places = sort_passes(x_raw, 1, 0, 0, X_PARTS[0])
-        for part, n in enumerate(X_PARTS):
-            grouped = transpose_units(sources_of(x_raw, places, 1, first, n))
-            if part + 1 < len(X_PARTS):
-                places = sort_passes(x_raw, 1, first + n, first + n, X_PARTS[part + 1])
+        def quantise(t):
+            step = steps[t]
+            n_words = len(step["columns"]) * tiles[step["tile"]][0] * P
+            if step["gate"] == "x":
+                first = step["columns"][0] * P
+                codes = x_codes[:, first : first + n_words]
+                scales = x_scales[:, first : first + n_words]
             else:
-                sort_step(0)
-            if before is not None:
-                quantise_x(before[0], before[1], before[2])
-            before = (grouped, first, n)
-            first += n
-        quantise_x(before[0], before[1], before[2])
+                codes_of[t] = quantised_pool.tile([P, n_words], U32, name="w_codes", align_bytes=64)
+                scales_of[t] = quantised_pool.tile([P, n_words], U8, name="w_scales", align_bytes=64)
+                codes, scales = codes_of[t][:], scales_of[t][:]
+            nc.vector.quantize_mx(out=codes.bitcast(FP8X4), scales=scales, in_=grouped_of[t][:])
+
+        sums = {}
+
+        def multiply(t):
+            step = steps[t]
+            key = (step["gate"], step["block"])
+            if step["gate"] == "x":
+                return
+            width = tiles[step["tile"]][0] * P
+            opens = key not in sums
+            if opens:
+                sums[key] = sum_pool.tile([P, width], F32, name="sums")
+            for g, q in enumerate(step["passes"]):
+                nc.tensor.matmul_mx(
+                    out=sums[key][:],
+                    lhsT=x_codes[:, q * P : (q + 1) * P].bitcast(FP8X4),
+                    lhsT_scale=x_scales[:, q * P : (q + 1) * P],
+                    rhs=codes_of[t][:, g * width : (g + 1) * width].bitcast(FP8X4),
+                    rhs_scale=scales_of[t][:, g * width : (g + 1) * width],
+                    start=(opens and g == 0),
+                    stop=(q == PASSES - 1),
+                )
 
         spread = {}
 
-        def spread_row_vectors():
+        def spread_two_row_vectors(first):
             names = list(row_vectors)
-            for first in range(0, len(names), 2):
-                bank = bank_pool.tile([P, 2 * H], BF16, name="bank")
-                pair = keep.tile([P, 2 * H], BF16, name="spread%d" % first)
-                for v in (0, 1):
-                    nc.tensor.matmul(
-                        out=bank[:, v * H : (v + 1) * H], lhsT=ones[:],
-                        rhs=vector_rows[:, (first + v) * H : (first + v + 1) * H],
-                        start=True, stop=True,
-                    )
-                    spread[names[first + v]] = pair[:, v * H : (v + 1) * H]
-                nc.vector.tensor_copy(out=pair[:], in_=bank[:])
+            bank = bank_pool.tile([P, 2 * H], BF16, name="bank")
+            pair = keep.tile([P, 2 * H], BF16, name="spread%d" % first)
+            for v in (0, 1):
+                nc.tensor.matmul(
+                    out=bank[:, v * H : (v + 1) * H], lhsT=ones[:],
+                    rhs=vector_rows[:, (first + v) * H : (first + v + 1) * H],
+                    start=True, stop=True,
+                )
+                spread[names[first + v]] = pair[:, v * H : (v + 1) * H]
+            nc.scalar.copy(out=pair[:], in_=bank[:])
 
         full = {}
         for name in (
-            "act_f", "act_i", "act_z", "act_o", "f_c", "f_n", "f_m", "denominator", "reciprocal", "n_t", "i_z",
-            "larger", "c_t", "m_t", "half_ratio", "h", "centred", "h_t",
+            "act_f", "act_i", "act_z", "act_o", "f_c", "f_n", "f_m", "denominator", "reciprocal",
+            "n_t", "i_z", "size_i_z", "c_t", "m_t", "half_ratio", "h", "centred", "h_t",
         ):
             full[name] = keep.tile([P, H], F32, name=name)
         stats = keep.tile([P, BLOCKS_PER_GATE, 6], F32, name="stats")
         function_of = {"f": ACT.Tanh, "i": ACT.Exp, "z": ACT.Tanh, "o": ACT.Tanh}
         scale_of = {"f": 0.5, "i": 1.0, "z": 1.0, "o": 0.5}
-        sums = {}
         biased = {}
 
-        def columns(block):
+        def columns_of(block):
             return slice(0, H) if block is None else slice(block * P, (block + 1) * P)
 
         def add_bias(gate, block):
-            cols = columns(block)
+            cols = columns_of(block)
             width = cols.stop - cols.start
             biased[(gate, block)] = small_pool.tile([P, width], F32, name="biased")
             nc.vector.tensor_add(
@@ -278,7 +303,7 @@ def tile_slstmcell_k_kernel(
 
         def apply_function(gate, block):
             nc.scalar.activation(
-                out=full["act_" + gate][:, columns(block)], in_=biased[(gate, block)][:],
+                out=full["act_" + gate][:, columns_of(block)], in_=biased[(gate, block)][:],
                 func=function_of[gate], scale=scale_of[gate],
             )
 
@@ -292,106 +317,108 @@ def tile_slstmcell_k_kernel(
 
         def new_n():
             nc.vector.tensor_add(out=full["n_t"][:], in0=full["f_n"][:], in1=full["act_i"][:])
-            nc.gpsimd.dma_start(out=out_2, in_=full["n_t"][:])
 
         def denominator():
-            stt("denominator", "act_i", DIV_EPS, full["f_n"][:], ALU.add, ALU.add)
+            nc.vector.tensor_scalar_add(out=full["denominator"][:], in0=full["n_t"][:], scalar1=DIV_EPS)
 
         def reciprocal(block):
-            cols = columns(block)
+            cols = columns_of(block)
             nc.vector.reciprocal(out=full["reciprocal"][:, cols], in_=full["denominator"][:, cols])
 
         def i_z():
             nc.vector.tensor_mul(out=full["i_z"][:], in0=full["act_i"][:], in1=full["act_z"][:])
+            nc.scalar.activation(out=full["size_i_z"][:], in_=full["i_z"][:], func=ACT.Abs)
 
         def new_c():
             nc.vector.tensor_add(out=full["c_t"][:], in0=full["f_c"][:], in1=full["i_z"][:])
-            nc.gpsimd.dma_start(out=out_1, in_=full["c_t"][:])
-
-        def larger():
-            nc.vector.tensor_max(out=full["larger"][:], in0=full["f_m"][:], in1=full["i_z"][:])
 
         def new_m():
-            stt("m_t", "i_z", -1.0, full["larger"][:], ALU.mult, ALU.max)
-            nc.gpsimd.dma_start(out=out_3, in_=full["m_t"][:])
+            nc.vector.tensor_max(out=full["m_t"][:], in0=full["f_m"][:], in1=full["size_i_z"][:])
 
         def half_ratio():
             stt("half_ratio", "c_t", 0.5, full["reciprocal"][:], ALU.mult, ALU.mult)
 
         def hidden(block):
-            cols = columns(block)
+            cols = columns_of(block)
             stt("h", "act_o", 1.0, full["half_ratio"][:, cols], ALU.add, ALU.mult, cols)
 
         def statistics(block):
-            nc.vector.bn_stats(out=stats[:, block, :], in_=full["h"][:, columns(block)])
+            nc.vector.bn_stats(out=stats[:, block, :], in_=full["h"][:, columns_of(block)])
 
         later = {
             "f": [lambda: forget("n"), lambda: forget("c"), lambda: forget("m")],
-            "i": [denominator, new_n] + [lambda block=block: reciprocal(block) for block in range(BLOCKS_PER_GATE)],
-            "z": [i_z, larger, new_c, new_m, half_ratio],
+            "i": [new_n, denominator] + [lambda block=block: reciprocal(block) for block in range(BLOCKS_PER_GATE)],
+            "z": [i_z, new_c, half_ratio, new_m],
         }
         waiting = []
-
-        loaded = RAW_BUFS - 1
         served = 0
-        grouped_of = {}
-        codes_of = {}
-        scales_of = {}
 
         def finished(t):
-            if 0 <= t < len(steps) and steps[t]["first"] + steps[t]["passes"] == PASSES:
+            if 0 <= t < len(steps) and steps[t]["passes"][-1] == PASSES - 1 and steps[t]["gate"] != "x":
                 return steps[t]["gate"], steps[t]["block"]
             return None
 
-        for t in range(len(steps) + MULTIPLY_LAG + 3):
+        done_sorts = []
+
+        def sort_up_to(t):
+            for step in steps[: t + 1]:
+                if step["sort"] not in done_sorts and any(c % GROUP < sorts[step["sort"]][3] for c in step["columns"]):
+                    sort(step["sort"])
+                    done_sorts.append(step["sort"])
+
+        multiplied = 0
+        quantised = 0
+        to_add = []
+        to_combine = []
+        sort_up_to(0)
+        for t in range(len(steps) + MULTIPLY_LAG + 2):
             if t < len(steps):
-                step = steps[t]
-                while loaded < step["tile"] + RAW_BUFS and loaded < len(tiles):
+                while loaded < len(tiles) and loaded < steps[t]["tile"] + RAW_BUFS:
                     load(loaded)
                     loaded += 1
-                grouped_of[t] = transpose_units(
-                    sources_of(raw_of[step["tile"]], places_of[t], step["rows"], step["column"], step["passes"])
-                )
-            sort_step(t + 1)
-            if 0 <= t - 1 < len(steps):
-                n_words = steps[t - 1]["rows"] * steps[t - 1]["passes"] * P
-                codes_of[t - 1] = quantised_pool.tile([P, n_words], U32, name="w_codes", align_bytes=64)
-                scales_of[t - 1] = quantised_pool.tile([P, n_words], U8, name="w_scales", align_bytes=64)
-                quantise(grouped_of[t - 1], codes_of[t - 1][:], scales_of[t - 1][:])
-            if t == 5:
-                spread_row_vectors()
-            m = t - MULTIPLY_LAG
-            if 0 <= m < len(steps):
-                step = steps[m]
-                key = (step["gate"], step["block"])
-                width = H if step["block"] is None else P
-                if step["first"] == 0:
-                    sums[key] = sum_pool.tile([P, width], F32, name="sums")
-                for g in range(step["passes"]):
-                    q = step["first"] + g
-                    nc.tensor.matmul_mx(
-                        out=sums[key][:],
-                        lhsT=x_codes[:, q * P : (q + 1) * P].bitcast(FP8X4),
-                        lhsT_scale=x_scales[:, q * P : (q + 1) * P],
-                        rhs=codes_of[m][:, g * width : (g + 1) * width].bitcast(FP8X4),
-                        rhs_scale=scales_of[m][:, g * width : (g + 1) * width],
-                        start=(q == 0),
-                        stop=(q == PASSES - 1),
-                    )
-            done = finished(m - 1)
-            if done is not None:
-                add_bias(done[0], done[1])
-                apply_function(done[0], done[1])
-            done = finished(m - 2)
-            if done is not None and done[1] is None:
-                waiting.extend(later[done[0]])
+                if SORT_FIRST:
+                    sort_up_to(t + SORT_AHEAD)
+                transpose(t)
+            while quantised <= min(t - QUANTISE_LAG if t < len(steps) else t, len(steps) - 1):
+                quantise(quantised)
+                quantised += 1
+            if not SORT_FIRST:
+                sort_up_to(t + SORT_AHEAD)
+            if t in SPREAD_STEPS:
+                spread_two_row_vectors(2 * SPREAD_STEPS.index(t))
+            closed = []
+            if t % MULTIPLY_RUN == MULTIPLY_RUN - 1 or t >= len(steps):
+                while multiplied <= min(t - MULTIPLY_LAG if t < len(steps) else t, len(steps) - 1):
+                    multiply(multiplied)
+                    if finished(multiplied) is not None:
+                        closed.append(finished(multiplied))
+                    multiplied += 1
+
+            for gate, block in to_combine:
+                if block is None:
+                    waiting.extend(later[gate])
             for turn in range(2 if len(waiting) - served > 2 else 1):
                 if served < len(waiting):
                     waiting[served]()
                     served += 1
-            if done is not None and done[1] is not None:
-                hidden(done[1])
-                statistics(done[1])
+            for gate, block in to_combine:
+                if block is not None:
+                    while served < len(waiting):
+                        waiting[served]()
+                        served += 1
+                    if block == 0:
+                        for out, name in ((out_2, "n_t"), (out_1, "c_t"), (out_3, "m_t")):
+                            nc.sync.dma_start(out=out, in_=full[name][:])
+                    hidden(block)
+                    statistics(block)
+            for gate, block in to_add:
+                add_bias(gate, block)
+                apply_function(gate, block)
+            to_combine = to_add
+            to_add = closed
+            for out, in_ in left_for_vector:
+                nc.vector.tensor_copy(out=out, in_=in_)
+            left_for_vector.clear()
 
         mean_var = keep.tile([P, 2], F32, name="mean_var")
         nc.vector.bn_aggr(out=mean_var[:], in_=stats[:].rearrange("p j s -> p (j s)"))

from contextlib import ExitStack

import concourse.mybir as mybir
from concourse.masks import make_identity

F32 = mybir.dt.float32
BF16 = mybir.dt.bfloat16
I32 = mybir.dt.int32
U32 = mybir.dt.uint32
U8 = mybir.dt.uint8
FP8X4 = mybir.dt.float8_e4m3fn_x4
ALU = mybir.AluOpType
ACT = mybir.ActivationFunctionType

P = 128
IN = 7680
H = 512
D = IN + H
LN_EPS = 1e-5
DIV_EPS = 1e-6

PACK = 4
K_PASS = P * PACK
PASSES = D // K_PASS
PASS_WORDS = K_PASS // 2
BLOCK = 32
BLOCKS_PER_GATE = H // P
UNITS_PER_BANK = 2

GROUP = 4
SORTED = (2, 2, 1, 1)
WIDE_GATES = ("f", "i", "z")
NARROW_GATE = "o"
X_LOADS = (2, 2, 4, 8)
X_STEPS = (4, 4, 4, 4)
VECTOR_BANK_STEPS = 6
TAPER = (8, 4, 4)
RAW_BUFS = 5
TRANSPOSE_BANKS = 6
QUANTISE_LAG = 2
MULTIPLY_LAG = 3
MULTIPLY_RUN = 2
SPREAD_STEPS = (8, 9, 10)
VECTOR_BANK = 3
EARLY_STEPS = 18
EARLY_BANK_STEPS = 2
EARLY_TILES = 0
SORT_AHEAD = 2
SORT_FIRST = False

FLOPS = 2 * P * D * 4 * H


def tile_slstmcell_k_kernel(
    tc, x, h_prev, c_prev, n_prev, m_prev, Wi, bi, Wf, bf, Wo, bo, Wz, bz, ln_gamma, ln_beta,
    out_0, out_1, out_2, out_3,
):
    nc = tc.nc
    weights = {"f": Wf, "i": Wi, "z": Wz, "o": Wo}
    row_vectors = {"f": bf, "i": bi, "z": bz, "o": bo, "gamma": ln_gamma, "beta": ln_beta}
    previous = {"c": c_prev, "n": n_prev, "m": m_prev}

    with ExitStack() as ctx:
        ctx.enter_context(tc.manual_schedule())
        keep = ctx.enter_context(tc.tile_pool(name="keep", bufs=1))
        raw_pool = ctx.enter_context(tc.tile_pool(name="raw", bufs=RAW_BUFS))
        sorted_pool = ctx.enter_context(tc.tile_pool(name="sorted", bufs=3))
        grouped_pool = ctx.enter_context(tc.tile_pool(name="grouped", bufs=4))
        quantised_pool = ctx.enter_context(tc.tile_pool(name="quantised", bufs=4))
        small_pool = ctx.enter_context(tc.tile_pool(name="small", bufs=2))
        bank_pool = ctx.enter_context(tc.psum_pool(name="banks", bufs=TRANSPOSE_BANKS))
        sum_pool = ctx.enter_context(tc.psum_pool(name="sums", bufs=2))

        tiles = []
        sorts = []
        steps = []

        def add_step(gate, block, columns, first, sort):
            steps.append({
                "gate": gate, "block": block, "tile": len(tiles), "columns": columns,
                "passes": [first + c for c in columns], "sort": sort,
            })

        pieces = []
        first = 0
        for n in X_LOADS:
            k0, k1 = first * K_PASS, min((first + n) * K_PASS, IN)
            pieces.append((k0, x[:, k0:k1]))
            first += n
        pieces.append((IN, h_prev))
        first = 0
        for n in X_STEPS:
            add_step("x", None, list(range(first, first + n)), 0, len(sorts))
            sorts.append((0, first, n, SORTED[first // GROUP]))
            first += n
        tiles.append((1, PASSES, pieces))
        half = GROUP // 2
        for gate in WIDE_GATES:
            for first in range(0, PASSES, GROUP):
                pieces = []
                early = len(tiles) <= EARLY_TILES
                for a, b in ((half, GROUP), (0, half)) if early else ((0, GROUP),):
                    for r in range(0, BLOCKS_PER_GATE, 2):
                        source = weights[gate][
                            r * P : (r + 2) * P, (first + a) * K_PASS : (first + b) * K_PASS
                        ]
                        pieces.append(((r * GROUP + a) * K_PASS, source))
                for columns in ([2, 3], [0, 1]) if early else ([0, 2], [1, 3]):
                    add_step(gate, None, columns, first, len(sorts))
                sorts.append((len(tiles), 0, GROUP, SORTED[first // GROUP]))
                tiles.append((BLOCKS_PER_GATE, GROUP, pieces))
        for block in range(BLOCKS_PER_GATE):
            rows = slice(block * P, (block + 1) * P)
            pieces = []
            first = 0
            for n in TAPER if block == BLOCKS_PER_GATE - 1 else (8, 8):
                pieces.append((first * K_PASS, weights[NARROW_GATE][rows, first * K_PASS : (first + n) * K_PASS]))
                add_step(NARROW_GATE, block, list(range(first, first + n)), 0, len(sorts))
                sorts.append((len(tiles), first, n, SORTED[first // GROUP]))
                first += n
            tiles.append((1, PASSES, pieces))

        raw_of = {}
        loaded = 0

        def load(number):
            n_rows, n_passes, pieces = tiles[number]
            raw = raw_pool.tile([P, n_rows * n_passes * K_PASS], BF16, name="raw")
            raw_of[number] = raw
            for column, source in pieces:
                rows, width = source.shape
                if rows == P:
                    nc.sync.dma_start(out=raw[:, column : column + width], in_=source)
                else:
                    start = column % (n_passes * K_PASS)
                    part = column // (n_passes * K_PASS)
                    parts = raw[:].rearrange("p (a k) -> p a k", a=n_rows)[:, part : part + 2, start : start + width]
                    nc.sync.dma_start(out=parts, in_=source.rearrange("(a p) k -> p a k", a=2))

        load(0)
        load(1)
        load(2)
        load(3)
        identity = keep.tile([P, P], F32, name="identity")
        make_identity(nc, identity[:])
        vector_rows = keep.tile([P, len(row_vectors) * H], BF16, name="vector_rows")
        nc.vector.memset(vector_rows[:].bitcast(I32), 0)
        for v, name in enumerate(row_vectors):
            nc.gpsimd.dma_start(
                out=vector_rows[0:1, v * H : (v + 1) * H], in_=row_vectors[name].unsqueeze(0)
            )
        previous_bf16 = {}
        for name in previous:
            previous_bf16[name] = keep.tile([P, H], BF16, name="previous_" + name)
            nc.gpsimd.dma_start(out=previous_bf16[name][:], in_=previous[name])
        for number in range(4, RAW_BUFS):
            load(number)
        loaded = RAW_BUFS

        ones = keep.tile([P, P], BF16, name="ones")
        nc.vector.memset(ones[:], 1.0)
        minus_half = keep.tile([P, 1], F32, name="minus_half")
        nc.vector.memset(minus_half[:], -0.5)
        table_warmer = keep.tile([P, 1], F32, name="table_warmer")
        nc.scalar.activation(out=table_warmer[:], in_=minus_half[:], func=ACT.Tanh)
        half_previous = {}
        for name in previous:
            half_previous[name] = keep.tile([P, H], F32, name="half_previous_" + name)
            nc.gpsimd.tensor_scalar(
                out=half_previous[name][:], in0=previous_bf16[name][:],
                scalar1=0.5, scalar2=0.0, op0=ALU.mult, op1=ALU.add,
            )

        sorted_of = {}

        def sort(s):
            number, column, n, n_sorted = sorts[s]
            n_rows, n_passes, pieces = tiles[number]
            n_groups = n // GROUP
            outer = n_rows * n_groups
            size = n_sorted * K_PASS
            out = sorted_pool.tile([P, outer * size], BF16, name="sorted")
            in_ = raw_of[number][:].rearrange("p (a k) -> p a k", k=GROUP * K_PASS)
            if n_rows == 1:
                in_ = in_[:, column // GROUP : column // GROUP + n_groups, :]
            in_ = in_[:, :, 0:size]
            nc.vector.tensor_copy(
                out=out[:].rearrange("p (a u b e) -> p a u b e", a=outer, u=2, e=BLOCK // 2),
                in_=in_.rearrange("p a (b u e) -> p a u b e", u=2, e=BLOCK // 2),
            )
            sorted_of[s] = out

        def words_of(step, c, r, u):
            n_rows, n_passes, pieces = tiles[step["tile"]]
            number, start, n, n_sorted = sorts[step["sort"]]
            if c % GROUP < n_sorted:
                part = r if n_rows > 1 else (c - start) // GROUP
                column = part * n_sorted * PASS_WORDS + u * n_sorted * P + c % GROUP * P
                return sorted_of[step["sort"]][:].bitcast(F32)[:, column : column + P]
            column = (r * n_passes + c) * PASS_WORDS
            return raw_of[step["tile"]][:].bitcast(F32)[:, column + u : column + PASS_WORDS : 2]

        grouped_of = {}
        left_for_vector = []

        def transpose(t):
            step = steps[t]
            n_rows = tiles[step["tile"]][0]
            units = [(c, r) for c in step["columns"] for r in range(n_rows)]
            grouped = grouped_pool.tile([P, len(units) * K_PASS], BF16, name="grouped", align_bytes=64)
            grouped_of[t] = grouped
            span = UNITS_PER_BANK * PASS_WORDS
            for b in range(len(units) // UNITS_PER_BANK):
                bank = bank_pool.tile([P, 2, UNITS_PER_BANK * P], F32, name="bank")
                for s in range(UNITS_PER_BANK):
                    c, r = units[b * UNITS_PER_BANK + s]
                    for u in range(2):
                        nc.tensor.transpose(bank[:, u, s * P : (s + 1) * P], words_of(step, c, r, u), identity[:])
                out = grouped[:].bitcast(F32)[:, b * span : (b + 1) * span].rearrange("p (c u) -> p c u", u=2)
                in_ = bank[:].rearrange("p u c -> p c u")
                every = EARLY_BANK_STEPS if t < EARLY_STEPS else VECTOR_BANK_STEPS
                if t % every == every - 1 and b == VECTOR_BANK:
                    left_for_vector.append((out, in_))
                else:
                    nc.scalar.copy(out=out, in_=in_)

        x_codes = keep.tile([P, PASSES * P], U32, name="x_codes", align_bytes=64)
        x_scales = keep.tile([P, PASSES * P], U8, name="x_scales", align_bytes=64)
        codes_of = {}
        scales_of = {}

        def quantise(t):
            step = steps[t]
            n_words = len(step["columns"]) * tiles[step["tile"]][0] * P
            if step["gate"] == "x":
                first = step["columns"][0] * P
                codes = x_codes[:, first : first + n_words]
                scales = x_scales[:, first : first + n_words]
            else:
                codes_of[t] = quantised_pool.tile([P, n_words], U32, name="w_codes", align_bytes=64)
                scales_of[t] = quantised_pool.tile([P, n_words], U8, name="w_scales", align_bytes=64)
                codes, scales = codes_of[t][:], scales_of[t][:]
            nc.vector.quantize_mx(out=codes.bitcast(FP8X4), scales=scales, in_=grouped_of[t][:])

        sums = {}

        def multiply(t):
            step = steps[t]
            key = (step["gate"], step["block"])
            if step["gate"] == "x":
                return
            width = tiles[step["tile"]][0] * P
            opens = key not in sums
            if opens:
                sums[key] = sum_pool.tile([P, width], F32, name="sums")
            for g, q in enumerate(step["passes"]):
                nc.tensor.matmul_mx(
                    out=sums[key][:],
                    lhsT=x_codes[:, q * P : (q + 1) * P].bitcast(FP8X4),
                    lhsT_scale=x_scales[:, q * P : (q + 1) * P],
                    rhs=codes_of[t][:, g * width : (g + 1) * width].bitcast(FP8X4),
                    rhs_scale=scales_of[t][:, g * width : (g + 1) * width],
                    start=(opens and g == 0),
                    stop=(q == PASSES - 1),
                )

        spread = {}

        def spread_two_row_vectors(first):
            names = list(row_vectors)
            bank = bank_pool.tile([P, 2 * H], BF16, name="bank")
            pair = keep.tile([P, 2 * H], BF16, name="spread%d" % first)
            for v in (0, 1):
                nc.tensor.matmul(
                    out=bank[:, v * H : (v + 1) * H], lhsT=ones[:],
                    rhs=vector_rows[:, (first + v) * H : (first + v + 1) * H],
                    start=True, stop=True,
                )
                spread[names[first + v]] = pair[:, v * H : (v + 1) * H]
            nc.scalar.copy(out=pair[:], in_=bank[:])

        full = {}
        for name in (
            "act_f", "act_i", "act_z", "act_o", "f_c", "f_n", "f_m", "denominator", "reciprocal",
            "n_t", "i_z", "size_i_z", "c_t", "m_t", "half_ratio", "h", "centred", "h_t",
        ):
            full[name] = keep.tile([P, H], F32, name=name)
        stats = keep.tile([P, BLOCKS_PER_GATE, 6], F32, name="stats")
        function_of = {"f": ACT.Tanh, "i": ACT.Exp, "z": ACT.Tanh, "o": ACT.Tanh}
        scale_of = {"f": 0.5, "i": 1.0, "z": 1.0, "o": 0.5}
        biased = {}

        def columns_of(block):
            return slice(0, H) if block is None else slice(block * P, (block + 1) * P)

        def add_bias(gate, block):
            cols = columns_of(block)
            width = cols.stop - cols.start
            biased[(gate, block)] = small_pool.tile([P, width], F32, name="biased")
            nc.vector.tensor_add(
                out=biased[(gate, block)][:], in0=sums[(gate, block)][:], in1=spread[gate][:, cols]
            )

        def apply_function(gate, block):
            nc.scalar.activation(
                out=full["act_" + gate][:, columns_of(block)], in_=biased[(gate, block)][:],
                func=function_of[gate], scale=scale_of[gate],
            )

        def stt(out, in0, scalar, in1, op0, op1, cols=slice(0, H)):
            nc.vector.scalar_tensor_tensor(
                out=full[out][:, cols], in0=full[in0][:, cols], scalar=scalar, in1=in1, op0=op0, op1=op1
            )

        def forget(name):
            stt("f_" + name, "act_f", 1.0, half_previous[name][:], ALU.add, ALU.mult)

        def new_n():
            nc.vector.tensor_add(out=full["n_t"][:], in0=full["f_n"][:], in1=full["act_i"][:])

        def denominator():
            nc.vector.tensor_scalar_add(out=full["denominator"][:], in0=full["n_t"][:], scalar1=DIV_EPS)

        def reciprocal(block):
            cols = columns_of(block)
            nc.vector.reciprocal(out=full["reciprocal"][:, cols], in_=full["denominator"][:, cols])

        def i_z():
            nc.vector.tensor_mul(out=full["i_z"][:], in0=full["act_i"][:], in1=full["act_z"][:])
            nc.scalar.activation(out=full["size_i_z"][:], in_=full["i_z"][:], func=ACT.Abs)

        def new_c():
            nc.vector.tensor_add(out=full["c_t"][:], in0=full["f_c"][:], in1=full["i_z"][:])

        def new_m():
            nc.vector.tensor_max(out=full["m_t"][:], in0=full["f_m"][:], in1=full["size_i_z"][:])

        def half_ratio():
            stt("half_ratio", "c_t", 0.5, full["reciprocal"][:], ALU.mult, ALU.mult)

        def hidden(block):
            cols = columns_of(block)
            stt("h", "act_o", 1.0, full["half_ratio"][:, cols], ALU.add, ALU.mult, cols)

        def statistics(block):
            nc.vector.bn_stats(out=stats[:, block, :], in_=full["h"][:, columns_of(block)])

        later = {
            "f": [lambda: forget("n"), lambda: forget("c"), lambda: forget("m")],
            "i": [new_n, denominator] + [lambda block=block: reciprocal(block) for block in range(BLOCKS_PER_GATE)],
            "z": [i_z, new_c, half_ratio, new_m],
        }
        waiting = []
        served = 0

        def finished(t):
            if 0 <= t < len(steps) and steps[t]["passes"][-1] == PASSES - 1 and steps[t]["gate"] != "x":
                return steps[t]["gate"], steps[t]["block"]
            return None

        done_sorts = []

        def sort_up_to(t):
            for step in steps[: t + 1]:
                if step["sort"] not in done_sorts and any(c % GROUP < sorts[step["sort"]][3] for c in step["columns"]):
                    sort(step["sort"])
                    done_sorts.append(step["sort"])

        multiplied = 0
        quantised = 0
        to_add = []
        to_combine = []
        sort_up_to(0)
        for t in range(len(steps) + MULTIPLY_LAG + 2):
            if t < len(steps):
                while loaded < len(tiles) and loaded < steps[t]["tile"] + RAW_BUFS:
                    load(loaded)
                    loaded += 1
                if SORT_FIRST:
                    sort_up_to(t + SORT_AHEAD)
                transpose(t)
            while quantised <= min(t - QUANTISE_LAG if t < len(steps) else t, len(steps) - 1):
                quantise(quantised)
                quantised += 1
            if not SORT_FIRST:
                sort_up_to(t + SORT_AHEAD)
            if t in SPREAD_STEPS:
                spread_two_row_vectors(2 * SPREAD_STEPS.index(t))
            closed = []
            if t % MULTIPLY_RUN == MULTIPLY_RUN - 1 or t >= len(steps):
                while multiplied <= min(t - MULTIPLY_LAG if t < len(steps) else t, len(steps) - 1):
                    multiply(multiplied)
                    if finished(multiplied) is not None:
                        closed.append(finished(multiplied))
                    multiplied += 1

            for gate, block in to_combine:
                if block is None:
                    waiting.extend(later[gate])
            for turn in range(2 if len(waiting) - served > 2 else 1):
                if served < len(waiting):
                    waiting[served]()
                    served += 1
            for gate, block in to_combine:
                if block is not None:
                    while served < len(waiting):
                        waiting[served]()
                        served += 1
                    if block == 0:
                        for out, name in ((out_2, "n_t"), (out_1, "c_t"), (out_3, "m_t")):
                            nc.sync.dma_start(out=out, in_=full[name][:])
                    hidden(block)
                    statistics(block)
            for gate, block in to_add:
                add_bias(gate, block)
                apply_function(gate, block)
            to_combine = to_add
            to_add = closed
            for out, in_ in left_for_vector:
                nc.vector.tensor_copy(out=out, in_=in_)
            left_for_vector.clear()

        mean_var = keep.tile([P, 2], F32, name="mean_var")
        nc.vector.bn_aggr(out=mean_var[:], in_=stats[:].rearrange("p j s -> p (j s)"))
        var_eps = keep.tile([P, 1], F32, name="var_eps")
        nc.vector.tensor_scalar_add(out=var_eps[:], in0=mean_var[:, 1:2], scalar1=LN_EPS)
        inv_std = keep.tile([P, 1], F32, name="inv_std")
        nc.gpsimd.tensor_tensor(out=inv_std[:], in0=var_eps[:], in1=minus_half[:], op=ALU.pow)
        nc.vector.scalar_tensor_tensor(
            out=full["centred"][:], in0=full["h"][:], scalar=mean_var[:, 0:1],
            in1=spread["gamma"], op0=ALU.subtract, op1=ALU.mult,
        )
        for part, queue in enumerate((nc.sync, nc.scalar)):
            cols = slice(part * H // 2, (part + 1) * H // 2)
            nc.vector.scalar_tensor_tensor(
                out=full["h_t"][:, cols], in0=full["centred"][:, cols], scalar=inv_std[:],
                in1=spread["beta"][:, cols], op0=ALU.mult, op1=ALU.add,
            )
            queue.dma_start(out=out_0[:, cols], in_=full["h_t"][:, cols])
